import numpy as np
import ml_dtypes


def mxq(x, axis, fmt="e4m3"):
    dtype, down = {"e4m3": (ml_dtypes.float8_e4m3fn, 7), "e5m2": (ml_dtypes.float8_e5m2, 14)}[fmt]
    v = np.moveaxis(np.asarray(x, np.float32).astype(ml_dtypes.bfloat16).astype(np.float64), axis, -1)
    blocks = v.reshape(v.shape[:-1] + (-1, 32))
    amax = np.abs(blocks).max(-1, keepdims=True)
    byte = np.maximum(np.where(amax > 0, np.frexp(amax)[1] - 1 + 127, 0) - down, 1)
    scale = np.exp2(byte - 127.0)
    codes = (blocks / scale).astype(np.float32).astype(dtype).astype(np.float64)
    return np.moveaxis((codes * scale).reshape(v.shape), -1, axis)


WIDE = False


def mx_kscale(k):
    if not WIDE:
        return np.ones(k)
    levels = np.array([10, -10, 5, -5, 0])
    if k % 512:
        return np.exp2(np.random.permutation(np.resize(levels, k // 32))).repeat(32)
    a = np.empty((k // 512, 16))
    for p in range(k // 512):
        a[p, :8] = np.random.permutation(np.resize(levels, 8))
        for g in range(8):
            far = levels[np.abs(levels - a[p, g]) >= 10]
            a[p, g + 8] = far[np.random.randint(len(far))]
    return np.exp2(a.ravel()).repeat(32)


BF16 = ml_dtypes.bfloat16


def bf(x):
    return np.asarray(x, np.float32).astype(BF16)


def f64(x):
    return np.asarray(x).astype(np.float64)


B, S, D, BD, K = 2, 768, 1024, 512, 128
T = B * S
TS = 3.0
GS = 2.0


def sigmoid(v):
    return 1.0 / (1.0 + np.exp(-v))


def setup_inputs():
    s = mx_kscale(T).reshape(B, S, 1)
    u = mx_kscale(D)
    x0 = bf(np.random.standard_normal((B, S, D)) * TS)
    si = bf(np.random.uniform(size=(B, S, K)))
    dec = bf(np.random.standard_normal((B, K, D)) * 0.35)
    w0 = bf(np.random.standard_normal((D, D)) / (TS * np.sqrt(D)))
    gb = bf(np.random.standard_normal(D) * 0.5)
    g = bf(np.random.standard_normal((B, S, D)) * np.exp2(np.random.randint(-6, 1, (B, S, 1))) * GS / s * u)
    flow = f64(si) @ f64(dec)
    z = f64(x0) @ f64(w0) + f64(gb)
    return {
        "token_embeddings": bf(f64(x0) * s),
        "splat_influences": si,
        "decoded": dec,
        "gate_W": bf(f64(w0) / u[None, :]),
        "gate_b": gb,
        "flow": np.asarray(flow, np.float32),
        "z": np.asarray(z, np.float32),
        "grad_out": g,
    }


def reference(token_embeddings, splat_influences, decoded, gate_W, gate_b, flow, z, grad_out):
    x = f64(token_embeddings).reshape(T, D)
    gate = sigmoid(f64(z))
    dz = (f64(grad_out) * f64(flow) * gate * (1.0 - gate)).reshape(T, D)
    dx = mxq(dz, 1, "e5m2") @ mxq(f64(gate_W), 1, "e4m3").T
    dw = mxq(x, 0, "e4m3").T @ mxq(dz, 0, "e5m2")
    return dx.reshape(B, S, D), dw

@@ -1,0 +1,322 @@
+from contextlib import ExitStack
+
+import concourse.mybir as mybir
+from concourse.masks import make_identity
+
+T, D = 1536, 1024
+FLOPS = 2 * 2 * T * D * D
+BYTES = 2 * T * D + 2 * D * D + 4 * T * D + 4 * T * D + 2 * T * D + 4 * T * D + 4 * D * D
+
+F32 = mybir.dt.float32
+BF16 = mybir.dt.bfloat16
+U32 = mybir.dt.uint32
+U8 = mybir.dt.uint8
+E4M3 = mybir.dt.float8_e4m3fn_x4
+E5M2 = mybir.dt.float8_e5m2_x4
+ACT = mybir.ActivationFunctionType
+ALU = mybir.AluOpType
+
+P = 128
+PACK = 4
+KP = 512
+NG = T // KP
+NH = D // KP
+PIECE = 1024
+
+
+def tile_splatinformationflow_pb_v_kernel(
+    tc, token_embeddings, splat_influences, decoded, gate_W, gate_b, flow, z, grad_out, out_0, out_1
+):
+    nc = tc.nc
+    by_pass = "(g p j) w -> p g j w"
+    xv = token_embeddings.flatten_outer_dims().rearrange(by_pass, p=P, j=PACK)
+    zv = z.flatten_outer_dims().rearrange(by_pass, p=P, j=PACK)
+    fv = flow.flatten_outer_dims().rearrange(by_pass, p=P, j=PACK)
+    gv = grad_out.flatten_outer_dims().rearrange(by_pass, p=P, j=PACK)
+    o0v = out_0.flatten_outer_dims().rearrange(by_pass, p=P, j=PACK)
+    wv = gate_W.rearrange("(a p) o -> p a o", p=P)
+    o1v = out_1.rearrange("(a p) o -> p a o", p=P)
+
+    with ExitStack() as ctx:
+        const = ctx.enter_context(tc.tile_pool(name="const", bufs=1))
+        keep = ctx.enter_context(tc.tile_pool(name="keep", bufs=1))
+        zin = ctx.enter_context(tc.tile_pool(name="zin", bufs=3))
+        fin = ctx.enter_context(tc.tile_pool(name="fin", bufs=3))
+        gin = ctx.enter_context(tc.tile_pool(name="gin", bufs=3))
+        xin = ctx.enter_context(tc.tile_pool(name="xin", bufs=2))
+        dzp = ctx.enter_context(tc.tile_pool(name="dzp", bufs=2))
+        lace = ctx.enter_context(tc.tile_pool(name="lace", bufs=2))
+        grpp = ctx.enter_context(tc.tile_pool(name="grpp", bufs=3))
+        st0 = ctx.enter_context(tc.tile_pool(name="st0", bufs=2))
+        st1 = ctx.enter_context(tc.tile_pool(name="st1", bufs=3))
+        tps = ctx.enter_context(tc.psum_pool(name="tps", bufs=2))
+        ps0 = ctx.enter_context(tc.psum_pool(name="ps0", bufs=2))
+        ps1 = ctx.enter_context(tc.psum_pool(name="ps1", bufs=4))
+
+        ident = const.tile([P, P], F32, name="ident")
+        make_identity(nc, ident[:])
+        neg_half = const.tile([P, 1], F32, name="neg_half")
+        nc.vector.memset(neg_half[:], -0.5)
+        warm = const.tile([P, 1], F32, name="warm")
+        nc.scalar.activation(out=warm[:], in_=neg_half[:], func=ACT.Sigmoid)
+
+        wraw = keep.tile([P, D // P, D], BF16, name="wraw")
+        wT_c = [keep.tile([P, D], U32, name="wT_c%d" % h, align_bytes=64) for h in range(NH)]
+        wT_s = [keep.tile([P, D], U8, name="wT_s%d" % h, align_bytes=64) for h in range(NH)]
+        x_c = [keep.tile([P, D], U32, name="x_c%d" % g, align_bytes=64) for g in range(NG)]
+        x_s = [keep.tile([P, D], U8, name="x_s%d" % g, align_bytes=64) for g in range(NG)]
+        d1_c = [[keep.tile([P, KP], U32, name="d1_c%d_%d" % (g, h), align_bytes=64) for h in range(NH)] for g in range(NG)]
+        d1_s = [[keep.tile([P, KP], U8, name="d1_s%d_%d" % (g, h), align_bytes=64) for h in range(NH)] for g in range(NG)]
+        dT_c = [[[keep.tile([P, 2 * P], U32, name="dT_c%d_%d_%d" % (g, a, h), align_bytes=64) for h in range(NH)] for a in range(2)] for g in range(NG)]
+        dT_s = [[[keep.tile([P, 2 * P], U8, name="dT_s%d_%d_%d" % (g, a, h), align_bytes=64) for h in range(NH)] for a in range(2)] for g in range(NG)]
+
+        zt = {}
+        ft = {}
+        gt = {}
+        xt = {}
+        dzb = {}
+
+        rects = [
+            (0, 0, 2, 0, D),
+            (0, 2, 2, 0, D),
+            (1, 0, 2, 0, D),
+            (1, 2, 2, 0, D),
+            (2, 0, 4, 0, KP),
+            (2, 0, 2, KP, KP),
+            (2, 2, 2, KP, KP),
+        ]
+
+        def load_z(r):
+            g, j0, nj, w0, nw = rects[r]
+            zt[r] = zin.tile([P, nj, nw], F32, name="zt", tag="zt")
+            cut = nj if r > 0 else 1
+            for js in range(0, nj, cut):
+                nc.sync.dma_start(out=zt[r][:, js : js + cut, :], in_=zv[:, g, j0 + js : j0 + js + cut, w0 : w0 + nw])
+
+        def load_f(r):
+            g, j0, nj, w0, nw = rects[r]
+            ft[r] = fin.tile([P, nj, nw], F32, name="ft", tag="ft")
+            cut = nj if r > 0 else 1
+            for js in range(0, nj, cut):
+                nc.sync.dma_start(out=ft[r][:, js : js + cut, :], in_=fv[:, g, j0 + js : j0 + js + cut, w0 : w0 + nw])
+
+        def load_g(g):
+            gt[g] = gin.tile([P, PACK, D], BF16, name="gt", tag="gt")
+            for js in range(0, PACK, 2):
+                nc.sync.dma_start(out=gt[g][:, js : js + 2, :], in_=gv[:, g, js : js + 2, :])
+
+        def load_x(g):
+            xt[g] = xin.tile([P, PACK, D], BF16, name="xt", tag="xt")
+            nc.sync.dma_start(out=xt[g][:], in_=xv[:, g, :, :])
+
+        def pieces(r):
+            g, j0, nj, w0, nw = rects[r]
+            step = PIECE // nw
+            return [(js, step) for js in range(0, nj, step)]
+
+        def act(r):
+            if r == 0:
+                for js, step in pieces(r):
+                    v = zt[r][:, js : js + step, :]
+                    nc.scalar.activation(out=v, in_=v, func=ACT.Sigmoid)
+                    nc.scalar.activation(out=v, in_=v, func=ACT.Square, bias=neg_half[:])
+                return
+            for js, step in pieces(r):
+                v = zt[r][:, js : js + step, :]
+                nc.scalar.activation(out=v, in_=v, func=ACT.Sigmoid)
+            for js, step in pieces(r):
+                v = zt[r][:, js : js + step, :]
+                nc.scalar.activation(out=v, in_=v, func=ACT.Square, bias=neg_half[:])
+
+        def vec(r):
+            g, j0, nj, w0, nw = rects[r]
+            if g not in dzb:
+                dzb[g] = dzp.tile([P, PACK, D], BF16, name="dzb", tag="dzb")
+            for js, step in pieces(r):
+                v = zt[r][:, js : js + step, :]
+                nc.vector.scalar_tensor_tensor(
+                    out=v, in0=v, scalar=0.25, in1=ft[r][:, js : js + step, :], op0=ALU.subtract, op1=ALU.mult
+                )
+            for js, step in pieces(r):
+                v = zt[r][:, js : js + step, :]
+                jlo = j0 + js
+                nc.vector.scalar_tensor_tensor(
+                    out=dzb[g][:, jlo : jlo + step, w0 : w0 + nw],
+                    in0=v,
+                    scalar=-1.0,
+                    in1=gt[g][:, jlo : jlo + step, w0 : w0 + nw],
+                    op0=ALU.mult,
+                    op1=ALU.mult,
+                )
+
+        def turn(words, rows, h, codes, scales, fmt, on_scalar):
+            bank = tps.tile([P, 2, 2, P], F32, name="bank", tag="bank")
+            for i in range(2):
+                for u in range(2):
+                    nc.tensor.transpose(
+                        bank[:, i, u, :], words[:, rows[i], 256 * h + u : 256 * (h + 1) : 2], ident[:]
+                    )
+            grp = grpp.tile([P, 2, P, PACK], BF16, name="grp", tag="grp", align_bytes=64)
+            if on_scalar:
+                nc.scalar.copy(out=grp[:].bitcast(F32), in_=bank[:].rearrange("m i u r -> m i r u"))
+            else:
+                nc.vector.tensor_copy(out=grp[:].bitcast(F32), in_=bank[:].rearrange("m i u r -> m i r u"))
+            nc.vector.quantize_mx(
+                out=codes.bitcast(fmt), scales=scales, in_=grp[:].rearrange("m i r t -> m (i r t)")
+            )
+
+        def turn_w(h, ip):
+            cols = slice(2 * P * ip, 2 * P * (ip + 1))
+            turn(wraw[:].bitcast(F32), (2 * ip, 2 * ip + 1), h, wT_c[h][:, cols], wT_s[h][:, cols], E4M3, ip % 2 == 0)
+
+        def turn_dz(g, a, h):
+            turn(dzb[g][:].bitcast(F32), (2 * a, 2 * a + 1), h, dT_c[g][a][h][:], dT_s[g][a][h][:], E5M2, True)
+
+        def lace_quant(src, codes, scales, fmt):
+            laced = lace.tile([P, KP, PACK], BF16, name="laced", tag="laced", align_bytes=64)
+            nc.vector.tensor_copy(
+                out=laced[:].rearrange("p (c i) t -> p c t i", i=4), in_=src.rearrange("p t (c i) -> p c t i", i=4)
+            )
+            nc.vector.quantize_mx(out=codes.bitcast(fmt), scales=scales, in_=laced[:].rearrange("p w t -> p (w t)"))
+
+        def road1(g, h):
+            lace_quant(dzb[g][:, :, KP * h : KP * (h + 1)], d1_c[g][h][:], d1_s[g][h][:], E5M2)
+
+        def xprep(g):
+            for h in range(NH):
+                cols = slice(KP * h, KP * (h + 1))
+                lace_quant(xt[g][:, :, cols], x_c[g][:, cols], x_s[g][:, cols], E4M3)
+
+        def evac(out, in_, on_scalar):
+            if on_scalar:
+                nc.scalar.copy(out=out, in_=in_)
+            else:
+                nc.vector.tensor_copy(out=out, in_=in_)
+
+        def out0(g, a, share):
+            o0t = st0.tile([P, 2, D], F32, name="o0t", tag="o0t")
+            for i in range(2):
+                rows = slice(P * i, P * (i + 1))
+                for n in range(NH):
+                    cols = slice(KP * n, KP * (n + 1))
+                    acc = ps0.tile([P, KP], F32, name="acc0", tag="acc0")
+                    for h in range(NH):
+                        nc.tensor.matmul_mx(
+                            out=acc[:],
+                            lhsT=dT_c[g][a][h][:, rows].bitcast(E5M2),
+                            lhsT_scale=dT_s[g][a][h][:, rows],
+                            rhs=wT_c[h][:, cols].bitcast(E4M3),
+                            rhs_scale=wT_s[h][:, cols],
+                            start=(h == 0),
+                            stop=(h == NH - 1),
+                        )
+                    evac(o0t[:, i, cols], acc[:], (not share) or n == 0)
+            nc.sync.dma_start(out=o0v[:, g, 2 * a : 2 * a + 2, :], in_=o0t[:])
+
+        def o1_mm(acc, ia, h, g):
+            rows = slice(P * ia, P * (ia + 1))
+            nc.tensor.matmul_mx(
+                out=acc[:],
+                lhsT=x_c[g][:, rows].bitcast(E4M3),
+                lhsT_scale=x_s[g][:, rows],
+                rhs=d1_c[g][h][:].bitcast(E5M2),
+                rhs_scale=d1_s[g][h][:],
+                start=(g == 0),
+                stop=(g == NG - 1),
+            )
+
+        def o1_open(h, ias):
+            accs = []
+            for ia in ias:
+                acc = ps1.tile([P, KP], F32, name="acc1", tag="acc1")
+                for g in range(NG - 1):
+                    o1_mm(acc, ia, h, g)
+                accs.append(acc)
+            return accs
+
+        def o1_close(h, ias, accs, share):
+            for k in range(0, len(ias), 2):
+                o1t = st1.tile([P, 2, KP], F32, name="o1t", tag="o1t")
+                for i in range(2):
+                    o1_mm(accs[k + i], ias[k + i], h, NG - 1)
+                    evac(o1t[:, i, :], accs[k + i][:], (not share) or i == 0)
+                nc.sync.dma_start(out=o1v[:, ias[k] : ias[k] + 2, KP * h : KP * (h + 1)], in_=o1t[:])
+
+        def o1_full(h, ias, share):
+            for k in range(0, len(ias), 2):
+                accs = o1_open(h, ias[k : k + 2])
+                o1_close(h, ias[k : k + 2], accs, share)
+
+        load_z(0)
+        load_f(0)
+        load_g(0)
+        load_z(1)
+        for a0 in range(0, D // P, 2):
+            nc.sync.dma_start(out=wraw[:, a0 : a0 + 2, :], in_=wv[:, a0 : a0 + 2, :])
+        load_f(1)
+        load_x(0)
+        load_z(2)
+        load_f(2)
+        load_g(1)
+        load_x(1)
+
+        act(0)
+        vec(0)
+        load_z(3)
+        load_f(3)
+        act(1)
+        for ip in range(4):
+            for h in range(NH):
+                turn_w(h, ip)
+        xprep(0)
+        load_x(2)
+        turn_dz(0, 0, 0)
+        turn_dz(0, 0, 1)
+        vec(1)
+        load_z(4)
+        load_f(4)
+        load_g(2)
+        act(2)
+        out0(0, 0, False)
+        turn_dz(0, 1, 0)
+        turn_dz(0, 1, 1)
+        road1(0, 0)
+        road1(0, 1)
+        vec(2)
+        load_z(5)
+        load_f(5)
+        act(3)
+        out0(0, 1, False)
+        xprep(1)
+        turn_dz(1, 0, 0)
+        turn_dz(1, 0, 1)
+        vec(3)
+        load_z(6)
+        load_f(6)
+        act(4)
+        out0(1, 0, False)
+        turn_dz(1, 1, 0)
+        turn_dz(1, 1, 1)
+        road1(1, 0)
+        road1(1, 1)
+        early = o1_open(0, [0, 1, 2, 3])
+        vec(4)
+        act(5)
+        out0(1, 1, False)
+        xprep(2)
+        road1(2, 0)
+        o1_close(0, [0, 1, 2, 3], early, False)
+        o1_full(0, [4, 5, 6, 7], False)
+        turn_dz(2, 0, 0)
+        turn_dz(2, 1, 0)
+        vec(5)
+        act(6)
+        early = o1_open(1, [0, 1, 2, 3])
+        turn_dz(2, 0, 1)
+        vec(6)
+        out0(2, 0, False)
+        road1(2, 1)
+        turn_dz(2, 1, 1)
+        o1_close(1, [0, 1, 2, 3], early, True)
+        out0(2, 1, True)
+        o1_full(1, [4, 5, 6, 7], True)

@@ -23,6 +23,16 @@ NG = T // KP
 NH = D // KP
 PIECE = 1024
 
+RECTS = [
+    (0, 0, 2, 0, 1024),
+    (0, 2, 2, 0, 1024),
+    (1, 0, 2, 0, 1024),
+    (1, 2, 2, 0, 1024),
+    (2, 0, 4, 0, 512),
+    (2, 0, 2, 512, 512),
+    (2, 2, 2, 512, 512),
+]
+
 
 def tile_splatinformationflow_pb_v_kernel(
     tc, token_embeddings, splat_influences, decoded, gate_W, gate_b, flow, z, grad_out, out_0, out_1
@@ -38,26 +48,18 @@ def tile_splatinformationflow_pb_v_kernel(
     o1v = out_1.rearrange("(a p) o -> p a o", p=P)
 
     with ExitStack() as ctx:
-        const = ctx.enter_context(tc.tile_pool(name="const", bufs=1))
         keep = ctx.enter_context(tc.tile_pool(name="keep", bufs=1))
-        zin = ctx.enter_context(tc.tile_pool(name="zin", bufs=3))
-        fin = ctx.enter_context(tc.tile_pool(name="fin", bufs=3))
-        gin = ctx.enter_context(tc.tile_pool(name="gin", bufs=3))
-        xin = ctx.enter_context(tc.tile_pool(name="xin", bufs=2))
-        dzp = ctx.enter_context(tc.tile_pool(name="dzp", bufs=2))
-        lace = ctx.enter_context(tc.tile_pool(name="lace", bufs=2))
+        lace = ctx.enter_context(tc.tile_pool(name="lace", bufs=3))
         grpp = ctx.enter_context(tc.tile_pool(name="grpp", bufs=3))
-        st0 = ctx.enter_context(tc.tile_pool(name="st0", bufs=2))
-        st1 = ctx.enter_context(tc.tile_pool(name="st1", bufs=3))
         tps = ctx.enter_context(tc.psum_pool(name="tps", bufs=2))
         ps0 = ctx.enter_context(tc.psum_pool(name="ps0", bufs=2))
         ps1 = ctx.enter_context(tc.psum_pool(name="ps1", bufs=4))
 
-        ident = const.tile([P, P], F32, name="ident")
+        ident = keep.tile([P, P], F32, name="ident")
         make_identity(nc, ident[:])
-        neg_half = const.tile([P, 1], F32, name="neg_half")
+        neg_half = keep.tile([P, 1], F32, name="neg_half")
         nc.vector.memset(neg_half[:], -0.5)
-        warm = const.tile([P, 1], F32, name="warm")
+        warm = keep.tile([P, 1], F32, name="warm")
         nc.scalar.activation(out=warm[:], in_=neg_half[:], func=ACT.Sigmoid)
 
         wraw = keep.tile([P, D // P, D], BF16, name="wraw")
@@ -69,154 +71,178 @@ def tile_splatinformationflow_pb_v_kernel(
         d1_s = [[keep.tile([P, KP], U8, name="d1_s%d_%d" % (g, h), align_bytes=64) for h in range(NH)] for g in range(NG)]
         dT_c = [[[keep.tile([P, 2 * P], U32, name="dT_c%d_%d_%d" % (g, a, h), align_bytes=64) for h in range(NH)] for a in range(2)] for g in range(NG)]
         dT_s = [[[keep.tile([P, 2 * P], U8, name="dT_s%d_%d_%d" % (g, a, h), align_bytes=64) for h in range(NH)] for a in range(2)] for g in range(NG)]
+        zt = [keep.tile([P, nj, nw], F32, name="zt%d" % r) for r, (g, j0, nj, w0, nw) in enumerate(RECTS)]
+        ft = [keep.tile([P, nj, nw], F32, name="ft%d" % r) for r, (g, j0, nj, w0, nw) in enumerate(RECTS)]
+        gt = [keep.tile([P, PACK, D], BF16, name="gt%d" % g) for g in range(NG)]
+        xt = [keep.tile([P, PACK, D], BF16, name="xt%d" % g) for g in range(NG)]
 
-        zt = {}
-        ft = {}
-        gt = {}
-        xt = {}
-        dzb = {}
+        o0t = {}
+        for g in range(2):
+            for a in range(2):
+                o0t[(g, a)] = ft[2 * g + a][:]
+        o0t[(2, 0)] = ft[4][:].rearrange("p a b -> p (a b)").rearrange("p (i c) -> p i c", i=2)
+        o0t[(2, 1)] = zt[4][:].rearrange("p a b -> p (a b)").rearrange("p (i c) -> p i c", i=2)
+        o1t = {}
+        for h in range(NH):
+            for ip in range(4):
+                o1t[(ip, h)] = zt[2 * h + ip // 2][:, ip % 2, :].rearrange("p (i c) -> p i c", i=2)
 
-        rects = [
-            (0, 0, 2, 0, D),
-            (0, 2, 2, 0, D),
-            (1, 0, 2, 0, D),
-            (1, 2, 2, 0, D),
-            (2, 0, 4, 0, KP),
-            (2, 0, 2, KP, KP),
-            (2, 2, 2, KP, KP),
-        ]
-
-        def load_z(r):
-            g, j0, nj, w0, nw = rects[r]
-            zt[r] = zin.tile([P, nj, nw], F32, name="zt", tag="zt")
-            cut = nj if r > 0 else 1
-            for js in range(0, nj, cut):
-                nc.sync.dma_start(out=zt[r][:, js : js + cut, :], in_=zv[:, g, j0 + js : j0 + js + cut, w0 : w0 + nw])
-
-        def load_f(r):
-            g, j0, nj, w0, nw = rects[r]
-            ft[r] = fin.tile([P, nj, nw], F32, name="ft", tag="ft")
-            cut = nj if r > 0 else 1
-            for js in range(0, nj, cut):
-                nc.sync.dma_start(out=ft[r][:, js : js + cut, :], in_=fv[:, g, j0 + js : j0 + js + cut, w0 : w0 + nw])
-
-        def load_g(g):
-            gt[g] = gin.tile([P, PACK, D], BF16, name="gt", tag="gt")
-            for js in range(0, PACK, 2):
-                nc.sync.dma_start(out=gt[g][:, js : js + 2, :], in_=gv[:, g, js : js + 2, :])
-
-        def load_x(g):
-            xt[g] = xin.tile([P, PACK, D], BF16, name="xt", tag="xt")
-            nc.sync.dma_start(out=xt[g][:], in_=xv[:, g, :, :])
+        bank = {}
+        grp = {}
+        laced = {}
+        acc0 = {}
+        acc1 = {}
 
         def pieces(r):
-            g, j0, nj, w0, nw = rects[r]
+            g, j0, nj, w0, nw = RECTS[r]
             step = PIECE // nw
             return [(js, step) for js in range(0, nj, step)]
 
-        def act(r):
-            if r == 0:
-                for js, step in pieces(r):
-                    v = zt[r][:, js : js + step, :]
-                    nc.scalar.activation(out=v, in_=v, func=ACT.Sigmoid)
-                    nc.scalar.activation(out=v, in_=v, func=ACT.Square, bias=neg_half[:])
-                return
-            for js, step in pieces(r):
-                v = zt[r][:, js : js + step, :]
-                nc.scalar.activation(out=v, in_=v, func=ACT.Sigmoid)
-            for js, step in pieces(r):
-                v = zt[r][:, js : js + step, :]
-                nc.scalar.activation(out=v, in_=v, func=ACT.Square, bias=neg_half[:])
-
-        def vec(r):
-            g, j0, nj, w0, nw = rects[r]
-            if g not in dzb:
-                dzb[g] = dzp.tile([P, PACK, D], BF16, name="dzb", tag="dzb")
-            for js, step in pieces(r):
-                v = zt[r][:, js : js + step, :]
-                nc.vector.scalar_tensor_tensor(
-                    out=v, in0=v, scalar=0.25, in1=ft[r][:, js : js + step, :], op0=ALU.subtract, op1=ALU.mult
-                )
-            for js, step in pieces(r):
-                v = zt[r][:, js : js + step, :]
-                jlo = j0 + js
-                nc.vector.scalar_tensor_tensor(
-                    out=dzb[g][:, jlo : jlo + step, w0 : w0 + nw],
-                    in0=v,
-                    scalar=-1.0,
-                    in1=gt[g][:, jlo : jlo + step, w0 : w0 + nw],
-                    op0=ALU.mult,
-                    op1=ALU.mult,
+        def load_rect(tiles, view, r, split):
+            g, j0, nj, w0, nw = RECTS[r]
+            cuts = pieces(r) if split else [(0, nj)]
+            for js, step in cuts:
+                nc.sync.dma_start(
+                    out=tiles[r][:, js : js + step, :], in_=view[:, g, j0 + js : j0 + js + step, w0 : w0 + nw]
                 )
 
-        def turn(words, rows, h, codes, scales, fmt, on_scalar):
-            bank = tps.tile([P, 2, 2, P], F32, name="bank", tag="bank")
-            for i in range(2):
-                for u in range(2):
-                    nc.tensor.transpose(
-                        bank[:, i, u, :], words[:, rows[i], 256 * h + u : 256 * (h + 1) : 2], ident[:]
-                    )
-            grp = grpp.tile([P, 2, P, PACK], BF16, name="grp", tag="grp", align_bytes=64)
-            if on_scalar:
-                nc.scalar.copy(out=grp[:].bitcast(F32), in_=bank[:].rearrange("m i u r -> m i r u"))
-            else:
-                nc.vector.tensor_copy(out=grp[:].bitcast(F32), in_=bank[:].rearrange("m i u r -> m i r u"))
-            nc.vector.quantize_mx(
-                out=codes.bitcast(fmt), scales=scales, in_=grp[:].rearrange("m i r t -> m (i r t)")
+        def load_z(r, split):
+            load_rect(zt, zv, r, split)
+
+        def load_f(r, split):
+            load_rect(ft, fv, r, split)
+
+        def load_g(g, a):
+            nc.sync.dma_start(out=gt[g][:, 2 * a : 2 * a + 2, :], in_=gv[:, g, 2 * a : 2 * a + 2, :])
+
+        def load_x(g):
+            nc.sync.dma_start(out=xt[g][:], in_=xv[:, g, :, :])
+
+        def load_w(a0):
+            nc.sync.dma_start(out=wraw[:, a0 : a0 + 2, :], in_=wv[:, a0 : a0 + 2, :])
+
+        def zpiece(r, p):
+            js, step = pieces(r)[p]
+            return zt[r][:, js : js + step, :]
+
+        def sig(r, p):
+            v = zpiece(r, p)
+            nc.scalar.activation(out=v, in_=v, func=ACT.Sigmoid)
+
+        def sq(r, p):
+            v = zpiece(r, p)
+            nc.scalar.activation(out=v, in_=v, func=ACT.Square, bias=neg_half[:])
+
+        def C(r, p):
+            js, step = pieces(r)[p]
+            v = zpiece(r, p)
+            nc.vector.scalar_tensor_tensor(
+                out=v, in0=v, scalar=0.25, in1=ft[r][:, js : js + step, :], op0=ALU.subtract, op1=ALU.mult
             )
 
-        def turn_w(h, ip):
-            cols = slice(2 * P * ip, 2 * P * (ip + 1))
-            turn(wraw[:].bitcast(F32), (2 * ip, 2 * ip + 1), h, wT_c[h][:, cols], wT_s[h][:, cols], E4M3, ip % 2 == 0)
-
-        def turn_dz(g, a, h):
-            turn(dzb[g][:].bitcast(F32), (2 * a, 2 * a + 1), h, dT_c[g][a][h][:], dT_s[g][a][h][:], E5M2, True)
-
-        def lace_quant(src, codes, scales, fmt):
-            laced = lace.tile([P, KP, PACK], BF16, name="laced", tag="laced", align_bytes=64)
-            nc.vector.tensor_copy(
-                out=laced[:].rearrange("p (c i) t -> p c t i", i=4), in_=src.rearrange("p t (c i) -> p c t i", i=4)
+        def Dz(r, p):
+            g, j0, nj, w0, nw = RECTS[r]
+            js, step = pieces(r)[p]
+            spot = gt[g][:, j0 + js : j0 + js + step, w0 : w0 + nw]
+            nc.vector.scalar_tensor_tensor(
+                out=spot, in0=zpiece(r, p), scalar=-1.0, in1=spot, op0=ALU.mult, op1=ALU.mult
             )
-            nc.vector.quantize_mx(out=codes.bitcast(fmt), scales=scales, in_=laced[:].rearrange("p w t -> p (w t)"))
 
-        def road1(g, h):
-            lace_quant(dzb[g][:, :, KP * h : KP * (h + 1)], d1_c[g][h][:], d1_s[g][h][:], E5M2)
-
-        def xprep(g):
-            for h in range(NH):
-                cols = slice(KP * h, KP * (h + 1))
-                lace_quant(xt[g][:, :, cols], x_c[g][:, cols], x_s[g][:, cols], E4M3)
-
-        def evac(out, in_, on_scalar):
-            if on_scalar:
+        def copy_on(eng, out, in_):
+            if eng == "S":
                 nc.scalar.copy(out=out, in_=in_)
             else:
                 nc.vector.tensor_copy(out=out, in_=in_)
 
-        def out0(g, a, share):
-            o0t = st0.tile([P, 2, D], F32, name="o0t", tag="o0t")
+        def turn_T(key, words, rows, h):
+            bank[key] = tps.tile([P, 2, 2, P], F32, name="bank", tag="bank")
             for i in range(2):
-                rows = slice(P * i, P * (i + 1))
-                for n in range(NH):
-                    cols = slice(KP * n, KP * (n + 1))
-                    acc = ps0.tile([P, KP], F32, name="acc0", tag="acc0")
-                    for h in range(NH):
-                        nc.tensor.matmul_mx(
-                            out=acc[:],
-                            lhsT=dT_c[g][a][h][:, rows].bitcast(E5M2),
-                            lhsT_scale=dT_s[g][a][h][:, rows],
-                            rhs=wT_c[h][:, cols].bitcast(E4M3),
-                            rhs_scale=wT_s[h][:, cols],
-                            start=(h == 0),
-                            stop=(h == NH - 1),
-                        )
-                    evac(o0t[:, i, cols], acc[:], (not share) or n == 0)
-            nc.sync.dma_start(out=o0v[:, g, 2 * a : 2 * a + 2, :], in_=o0t[:])
+                for u in range(2):
+                    nc.tensor.transpose(
+                        bank[key][:, i, u, :], words[:, rows[i], 256 * h + u : 256 * (h + 1) : 2], ident[:]
+                    )
 
-        def o1_mm(acc, ia, h, g):
+        def turn_C(key, eng):
+            grp[key] = grpp.tile([P, 2, P, PACK], BF16, name="grp", tag="grp", align_bytes=64)
+            copy_on(eng, grp[key][:].bitcast(F32), bank[key][:].rearrange("m i u r -> m i r u"))
+
+        def turn_Q(key, codes, scales, fmt):
+            nc.vector.quantize_mx(
+                out=codes.bitcast(fmt), scales=scales, in_=grp[key][:].rearrange("m i r t -> m (i r t)")
+            )
+
+        def wT(h, ip):
+            turn_T(("w", h, ip), wraw[:].bitcast(F32), (2 * ip, 2 * ip + 1), h)
+
+        def wC(h, ip, eng):
+            turn_C(("w", h, ip), eng)
+
+        def wQ(h, ip):
+            cols = slice(2 * P * ip, 2 * P * (ip + 1))
+            turn_Q(("w", h, ip), wT_c[h][:, cols], wT_s[h][:, cols], E4M3)
+
+        def dT(g, a, h):
+            turn_T((g, a, h), gt[g][:].bitcast(F32), (2 * a, 2 * a + 1), h)
+
+        def dC(g, a, h, eng):
+            turn_C((g, a, h), eng)
+
+        def dQ(g, a, h):
+            turn_Q((g, a, h), dT_c[g][a][h][:], dT_s[g][a][h][:], E5M2)
+
+        def lace_copy(key, src, eng):
+            laced[key] = lace.tile([P, KP, PACK], BF16, name="laced", tag="laced", align_bytes=64)
+            copy_on(
+                eng,
+                laced[key][:].rearrange("p (c i) t -> p c t i", i=4),
+                src.rearrange("p t (c i) -> p c t i", i=4),
+            )
+
+        def lace_quant(key, codes, scales, fmt):
+            nc.vector.quantize_mx(
+                out=codes.bitcast(fmt), scales=scales, in_=laced[key][:].rearrange("p w t -> p (w t)")
+            )
+
+        def lD(g, h):
+            lace_copy(("d", g, h), gt[g][:, :, KP * h : KP * (h + 1)], "V")
+
+        def qD(g, h):
+            lace_quant(("d", g, h), d1_c[g][h][:], d1_s[g][h][:], E5M2)
+
+        def lX(g, h, eng):
+            lace_copy(("x", g, h), xt[g][:, :, KP * h : KP * (h + 1)], eng)
+
+        def qX(g, h):
+            cols = slice(KP * h, KP * (h + 1))
+            lace_quant(("x", g, h), x_c[g][:, cols], x_s[g][:, cols], E4M3)
+
+        def mm0(g, a, i, n, h):
+            if h == 0:
+                acc0[(g, a, i, n)] = ps0.tile([P, KP], F32, name="acc0", tag="acc0")
+            rows = slice(P * i, P * (i + 1))
+            cols = slice(KP * n, KP * (n + 1))
+            nc.tensor.matmul_mx(
+                out=acc0[(g, a, i, n)][:],
+                lhsT=dT_c[g][a][h][:, rows].bitcast(E5M2),
+                lhsT_scale=dT_s[g][a][h][:, rows],
+                rhs=wT_c[h][:, cols].bitcast(E4M3),
+                rhs_scale=wT_s[h][:, cols],
+                start=(h == 0),
+                stop=(h == NH - 1),
+            )
+
+        def ev0(g, a, i, n, eng):
+            copy_on(eng, o0t[(g, a)][:, i, KP * n : KP * (n + 1)], acc0[(g, a, i, n)][:])
+
+        def s0(g, a):
+            nc.sync.dma_start(out=o0v[:, g, 2 * a : 2 * a + 2, :], in_=o0t[(g, a)])
+
+        def mm1(ia, h, g):
+            if g == 0:
+                acc1[(ia, h)] = ps1.tile([P, KP], F32, name="acc1", tag="acc1")
             rows = slice(P * ia, P * (ia + 1))
             nc.tensor.matmul_mx(
-                out=acc[:],
+                out=acc1[(ia, h)][:],
                 lhsT=x_c[g][:, rows].bitcast(E4M3),
                 lhsT_scale=x_s[g][:, rows],
                 rhs=d1_c[g][h][:].bitcast(E5M2),
@@ -225,98 +251,319 @@ def tile_splatinformationflow_pb_v_kernel(
                 stop=(g == NG - 1),
             )
 
-        def o1_open(h, ias):
-            accs = []
-            for ia in ias:
-                acc = ps1.tile([P, KP], F32, name="acc1", tag="acc1")
-                for g in range(NG - 1):
-                    o1_mm(acc, ia, h, g)
-                accs.append(acc)
-            return accs
+        def ev1(ia, h, eng):
+            copy_on(eng, o1t[(ia // 2, h)][:, ia % 2, :], acc1[(ia, h)][:])
 
-        def o1_close(h, ias, accs, share):
-            for k in range(0, len(ias), 2):
-                o1t = st1.tile([P, 2, KP], F32, name="o1t", tag="o1t")
-                for i in range(2):
-                    o1_mm(accs[k + i], ias[k + i], h, NG - 1)
-                    evac(o1t[:, i, :], accs[k + i][:], (not share) or i == 0)
-                nc.sync.dma_start(out=o1v[:, ias[k] : ias[k] + 2, KP * h : KP * (h + 1)], in_=o1t[:])
+        def s1(ip, h):
+            nc.sync.dma_start(out=o1v[:, 2 * ip : 2 * ip + 2, KP * h : KP * (h + 1)], in_=o1t[(ip, h)])
 
-        def o1_full(h, ias, share):
-            for k in range(0, len(ias), 2):
-                accs = o1_open(h, ias[k : k + 2])
-                o1_close(h, ias[k : k + 2], accs, share)
-
-        load_z(0)
-        load_f(0)
-        load_g(0)
-        load_z(1)
-        for a0 in range(0, D // P, 2):
-            nc.sync.dma_start(out=wraw[:, a0 : a0 + 2, :], in_=wv[:, a0 : a0 + 2, :])
-        load_f(1)
-        load_x(0)
-        load_z(2)
-        load_f(2)
-        load_g(1)
-        load_x(1)
-
-        act(0)
-        vec(0)
-        load_z(3)
-        load_f(3)
-        act(1)
-        for ip in range(4):
-            for h in range(NH):
-                turn_w(h, ip)
-        xprep(0)
-        load_x(2)
-        turn_dz(0, 0, 0)
-        turn_dz(0, 0, 1)
-        vec(1)
-        load_z(4)
-        load_f(4)
-        load_g(2)
-        act(2)
-        out0(0, 0, False)
-        turn_dz(0, 1, 0)
-        turn_dz(0, 1, 1)
-        road1(0, 0)
-        road1(0, 1)
-        vec(2)
-        load_z(5)
-        load_f(5)
-        act(3)
-        out0(0, 1, False)
-        xprep(1)
-        turn_dz(1, 0, 0)
-        turn_dz(1, 0, 1)
-        vec(3)
-        load_z(6)
-        load_f(6)
-        act(4)
-        out0(1, 0, False)
-        turn_dz(1, 1, 0)
-        turn_dz(1, 1, 1)
-        road1(1, 0)
-        road1(1, 1)
-        early = o1_open(0, [0, 1, 2, 3])
-        vec(4)
-        act(5)
-        out0(1, 1, False)
-        xprep(2)
-        road1(2, 0)
-        o1_close(0, [0, 1, 2, 3], early, False)
-        o1_full(0, [4, 5, 6, 7], False)
-        turn_dz(2, 0, 0)
-        turn_dz(2, 1, 0)
-        vec(5)
-        act(6)
-        early = o1_open(1, [0, 1, 2, 3])
-        turn_dz(2, 0, 1)
-        vec(6)
-        out0(2, 0, False)
-        road1(2, 1)
-        turn_dz(2, 1, 1)
-        o1_close(1, [0, 1, 2, 3], early, True)
-        out0(2, 1, True)
-        o1_full(1, [4, 5, 6, 7], True)
+        with tc.manual_schedule():
+            load_z(0, True)
+            load_f(0, True)
+            sig(0, 0)
+            sig(0, 1)
+            load_g(0, 0)
+            sq(0, 0)
+            load_w(0)
+            sq(0, 1)
+            C(0, 0)
+            load_w(2)
+            C(0, 1)
+            load_w(4)
+            Dz(0, 0)
+            wT(0, 0)
+            wT(1, 0)
+            wC(0, 0, "S")
+            load_w(6)
+            Dz(0, 1)
+            wC(1, 0, "S")
+            wT(0, 1)
+            wT(1, 1)
+            wC(0, 1, "S")
+            load_x(0)
+            wQ(0, 0)
+            wQ(1, 0)
+            wC(1, 1, "S")
+            wT(0, 2)
+            wQ(0, 1)
+            wC(0, 2, "S")
+            wQ(1, 1)
+            wT(1, 2)
+            wC(1, 2, "S")
+            wQ(0, 2)
+            wT(0, 3)
+            load_z(1, False)
+            wC(0, 3, "S")
+            wQ(1, 2)
+            wT(1, 3)
+            wC(1, 3, "S")
+            wQ(0, 3)
+            dT(0, 0, 0)
+            dC(0, 0, 0, "S")
+            wQ(1, 3)
+            dT(0, 0, 1)
+            lX(0, 0, "V")
+            dC(0, 0, 1, "S")
+            load_f(1, False)
+            lX(0, 1, "V")
+            sig(1, 0)
+            load_g(0, 1)
+            qX(0, 0)
+            sig(1, 1)
+            dQ(0, 0, 0)
+            qX(0, 1)
+            load_z(2, False)
+            mm0(0, 0, 0, 0, 0)
+            mm0(0, 0, 0, 1, 0)
+            dQ(0, 0, 1)
+            sq(1, 0)
+            mm0(0, 0, 0, 0, 1)
+            mm0(0, 0, 0, 1, 1)
+            sq(1, 1)
+            C(1, 0)
+            load_f(2, False)
+            ev0(0, 0, 0, 0, "S")
+            C(1, 1)
+            ev0(0, 0, 0, 1, "S")
+            mm0(0, 0, 1, 0, 0)
+            mm0(0, 0, 1, 0, 1)
+            sig(2, 0)
+            Dz(1, 0)
+            mm0(0, 0, 1, 1, 0)
+            mm0(0, 0, 1, 1, 1)
+            load_g(1, 0)
+            ev0(0, 0, 1, 0, "S")
+            Dz(1, 1)
+            load_x(1)
+            ev0(0, 0, 1, 1, "S")
+            sq(2, 0)
+            lD(0, 0)
+            dT(0, 1, 0)
+            dT(0, 1, 1)
+            sig(2, 1)
+            load_z(3, False)
+            C(2, 0)
+            dC(0, 1, 0, "S")
+            qD(0, 0)
+            sq(2, 1)
+            dQ(0, 1, 0)
+            mm1(0, 0, 0)
+            lX(1, 0, "V")
+            load_f(3, False)
+            mm0(0, 1, 0, 0, 0)
+            dC(0, 1, 1, "S")
+            mm0(0, 1, 0, 1, 0)
+            mm1(1, 0, 0)
+            mm1(2, 0, 0)
+            mm1(3, 0, 0)
+            lX(1, 1, "V")
+            sig(3, 0)
+            load_g(1, 1)
+            qX(1, 0)
+            sig(3, 1)
+            qX(1, 1)
+            load_z(4, False)
+            dQ(0, 1, 1)
+            Dz(2, 0)
+            sq(3, 0)
+            mm0(0, 1, 0, 0, 1)
+            mm0(0, 1, 0, 1, 1)
+            C(2, 1)
+            ev0(0, 1, 0, 0, "S")
+            ev0(0, 1, 0, 1, "S")
+            mm0(0, 1, 1, 0, 0)
+            load_f(4, False)
+            mm0(0, 1, 1, 0, 1)
+            C(3, 0)
+            sq(3, 1)
+            mm0(0, 1, 1, 1, 0)
+            mm0(0, 1, 1, 1, 1)
+            Dz(2, 1)
+            ev0(0, 1, 1, 0, "S")
+            ev0(0, 1, 1, 1, "S")
+            load_g(2, 0)
+            Dz(3, 0)
+            sig(4, 0)
+            dT(1, 0, 0)
+            dT(1, 0, 1)
+            load_g(2, 1)
+            C(3, 1)
+            dC(1, 0, 0, "S")
+            dC(1, 0, 1, "S")
+            load_x(2)
+            dQ(1, 0, 0)
+            sq(4, 0)
+            dQ(1, 0, 1)
+            mm0(1, 0, 0, 0, 0)
+            Dz(3, 1)
+            mm0(1, 0, 0, 0, 1)
+            mm0(1, 0, 0, 1, 0)
+            sig(4, 1)
+            mm0(1, 0, 0, 1, 1)
+            C(4, 0)
+            dT(1, 1, 0)
+            load_z(5, False)
+            ev0(1, 0, 0, 0, "S")
+            dT(1, 1, 1)
+            ev0(1, 0, 0, 1, "S")
+            lD(1, 0)
+            mm0(1, 0, 1, 0, 0)
+            mm0(1, 0, 1, 0, 1)
+            sq(4, 1)
+            load_f(5, False)
+            mm0(1, 0, 1, 1, 0)
+            mm0(1, 0, 1, 1, 1)
+            lX(2, 0, "V")
+            ev0(1, 0, 1, 0, "S")
+            load_z(6, False)
+            ev0(1, 0, 1, 1, "S")
+            lX(2, 1, "V")
+            dC(1, 1, 0, "S")
+            load_f(6, False)
+            dC(1, 1, 1, "S")
+            sig(5, 0)
+            qX(2, 0)
+            s0(0, 0)
+            qX(2, 1)
+            sig(6, 0)
+            dQ(1, 1, 0)
+            dQ(1, 1, 1)
+            mm0(1, 1, 0, 0, 0)
+            Dz(4, 0)
+            mm0(1, 1, 0, 0, 1)
+            sq(5, 0)
+            mm0(1, 1, 0, 1, 0)
+            mm0(1, 1, 0, 1, 1)
+            s0(0, 1)
+            qD(1, 0)
+            dT(2, 0, 0)
+            ev0(1, 1, 0, 0, "S")
+            C(4, 1)
+            ev0(1, 1, 0, 1, "S")
+            mm1(0, 0, 1)
+            mm0(1, 1, 1, 0, 0)
+            dC(2, 0, 0, "S")
+            mm0(1, 1, 1, 0, 1)
+            C(5, 0)
+            mm0(1, 1, 1, 1, 0)
+            ev0(1, 1, 1, 0, "S")
+            s0(1, 0)
+            mm0(1, 1, 1, 1, 1)
+            mm1(1, 0, 1)
+            ev0(1, 1, 1, 1, "S")
+            mm1(2, 0, 1)
+            dQ(2, 0, 0)
+            mm1(3, 0, 1)
+            sq(6, 0)
+            Dz(4, 1)
+            mm0(2, 0, 0, 0, 0)
+            mm0(2, 0, 0, 1, 0)
+            s0(1, 1)
+            Dz(5, 0)
+            dT(2, 1, 0)
+            dC(2, 1, 0, "S")
+            lD(2, 0)
+            dT(2, 0, 1)
+            dC(2, 0, 1, "S")
+            dQ(2, 1, 0)
+            qD(2, 0)
+            lD(0, 1)
+            mm1(0, 0, 2)
+            mm1(1, 0, 2)
+            ev1(0, 0, "S")
+            mm1(2, 0, 2)
+            mm1(3, 0, 2)
+            ev1(1, 0, "S")
+            lD(1, 1)
+            mm1(4, 0, 0)
+            mm1(4, 0, 1)
+            ev1(2, 0, "S")
+            s1(0, 0)
+            mm1(4, 0, 2)
+            mm1(5, 0, 0)
+            ev1(3, 0, "S")
+            mm1(5, 0, 1)
+            dQ(2, 0, 1)
+            mm1(5, 0, 2)
+            ev1(4, 0, "S")
+            qD(0, 1)
+            mm1(6, 0, 0)
+            s1(1, 0)
+            mm1(6, 0, 1)
+            ev1(5, 0, "S")
+            qD(1, 1)
+            mm1(6, 0, 2)
+            mm1(7, 0, 0)
+            ev1(6, 0, "S")
+            mm1(7, 0, 1)
+            C(6, 0)
+            s1(2, 0)
+            mm1(7, 0, 2)
+            mm1(0, 1, 0)
+            ev1(7, 0, "S")
+            mm1(1, 1, 0)
+            mm1(2, 1, 0)
+            Dz(6, 0)
+            mm1(3, 1, 0)
+            s1(3, 0)
+            mm1(0, 1, 1)
+            mm1(1, 1, 1)
+            mm1(2, 1, 1)
+            mm1(3, 1, 1)
+            lD(2, 1)
+            mm0(2, 0, 0, 0, 1)
+            mm0(2, 0, 0, 1, 1)
+            ev0(2, 0, 0, 0, "S")
+            dT(2, 1, 1)
+            ev0(2, 0, 0, 1, "V")
+            mm0(2, 0, 1, 0, 0)
+            mm0(2, 0, 1, 0, 1)
+            qD(2, 1)
+            ev0(2, 0, 1, 0, "S")
+            mm0(2, 0, 1, 1, 0)
+            dC(2, 1, 1, "S")
+            mm0(2, 0, 1, 1, 1)
+            mm1(0, 1, 2)
+            ev0(2, 0, 1, 1, "V")
+            mm1(1, 1, 2)
+            ev1(0, 1, "S")
+            mm1(2, 1, 2)
+            dQ(2, 1, 1)
+            s0(2, 0)
+            mm1(3, 1, 2)
+            ev1(2, 1, "S")
+            ev1(1, 1, "V")
+            mm1(4, 1, 0)
+            mm1(4, 1, 1)
+            ev1(3, 1, "V")
+            mm1(4, 1, 2)
+            mm1(5, 1, 0)
+            ev1(4, 1, "S")
+            mm1(5, 1, 1)
+            mm1(5, 1, 2)
+            mm1(6, 1, 0)
+            ev1(5, 1, "V")
+            s1(0, 1)
+            mm1(6, 1, 1)
+            mm1(6, 1, 2)
+            mm1(7, 1, 0)
+            ev1(6, 1, "S")
+            mm1(7, 1, 1)
+            mm1(7, 1, 2)
+            s1(1, 1)
+            mm0(2, 1, 0, 0, 0)
+            ev1(7, 1, "V")
+            mm0(2, 1, 0, 0, 1)
+            mm0(2, 1, 0, 1, 0)
+            ev0(2, 1, 0, 0, "S")
+            mm0(2, 1, 0, 1, 1)
+            s1(2, 1)
+            ev0(2, 1, 0, 1, "V")
+            mm0(2, 1, 1, 0, 0)
+            mm0(2, 1, 1, 0, 1)
+            mm0(2, 1, 1, 1, 0)
+            ev0(2, 1, 1, 0, "S")
+            mm0(2, 1, 1, 1, 1)
+            s1(3, 1)
+            ev0(2, 1, 1, 1, "V")
+            s0(2, 1)

@@ -3,9 +3,9 @@ from contextlib import ExitStack
 import concourse.mybir as mybir
 from concourse.masks import make_identity
 
-T, D = 1536, 1024
-FLOPS = 2 * 2 * T * D * D
-BYTES = 2 * T * D + 2 * D * D + 4 * T * D + 4 * T * D + 2 * T * D + 4 * T * D + 4 * D * D
+TOKENS, FEATURES = 1536, 1024
+FLOPS = 2 * 2 * TOKENS * FEATURES * FEATURES
+BYTES = (2 + 2 + 4 + 4 + 4) * TOKENS * FEATURES + (2 + 4) * FEATURES * FEATURES
 
 F32 = mybir.dt.float32
 BF16 = mybir.dt.bfloat16
@@ -18,19 +18,30 @@ ALU = mybir.AluOpType
 
 P = 128
 PACK = 4
-KP = 512
-NG = T // KP
-NH = D // KP
-PIECE = 1024
+HALF = P * PACK
+GROUPS = TOKENS // HALF
+HALVES = FEATURES // HALF
+WORDS = HALF // 2
+W_TILES = FEATURES // P
+RUN = 4
 
-RECTS = [
-    (0, 0, 2, 0, 1024),
-    (0, 2, 2, 0, 1024),
-    (1, 0, 2, 0, 1024),
-    (1, 2, 2, 0, 1024),
-    (2, 0, 4, 0, 512),
-    (2, 0, 2, 512, 512),
-    (2, 2, 2, 512, 512),
+PANELS = [
+    (0, 0, 2, 0, FEATURES),
+    (0, 2, 2, 0, FEATURES),
+    (1, 0, 2, 0, FEATURES),
+    (1, 2, 2, 0, FEATURES),
+    (2, 0, 4, 0, HALF),
+    (2, 0, 2, HALF, HALF),
+    (2, 2, 2, HALF, HALF),
+]
+PIECES = [
+    [(0, 1, 0, HALF), (0, 1, HALF, HALF), (1, 1, 0, FEATURES)],
+    [(0, 1, 0, FEATURES), (1, 1, 0, FEATURES)],
+    [(0, 1, 0, FEATURES), (1, 1, 0, FEATURES)],
+    [(0, 1, 0, FEATURES), (1, 1, 0, FEATURES)],
+    [(0, 2, 0, HALF), (2, 2, 0, HALF)],
+    [(0, 2, 0, HALF)],
+    [(0, 2, 0, HALF)],
 ]
 
 
@@ -38,532 +49,484 @@ def tile_splatinformationflow_pb_v_kernel(
     tc, token_embeddings, splat_influences, decoded, gate_W, gate_b, flow, z, grad_out, out_0, out_1
 ):
     nc = tc.nc
-    by_pass = "(g p j) w -> p g j w"
-    xv = token_embeddings.flatten_outer_dims().rearrange(by_pass, p=P, j=PACK)
-    zv = z.flatten_outer_dims().rearrange(by_pass, p=P, j=PACK)
-    fv = flow.flatten_outer_dims().rearrange(by_pass, p=P, j=PACK)
-    gv = grad_out.flatten_outer_dims().rearrange(by_pass, p=P, j=PACK)
-    o0v = out_0.flatten_outer_dims().rearrange(by_pass, p=P, j=PACK)
-    wv = gate_W.rearrange("(a p) o -> p a o", p=P)
-    o1v = out_1.rearrange("(a p) o -> p a o", p=P)
+
+    by_group = "(g p j) w -> p g j w"
+    x_hbm = token_embeddings.flatten_outer_dims().rearrange(by_group, p=P, j=PACK)
+    z_hbm = z.flatten_outer_dims().rearrange(by_group, p=P, j=PACK)
+    flow_hbm = flow.flatten_outer_dims().rearrange(by_group, p=P, j=PACK)
+    grad_hbm = grad_out.flatten_outer_dims().rearrange(by_group, p=P, j=PACK)
+    dx_hbm = out_0.flatten_outer_dims().rearrange(by_group, p=P, j=PACK)
+    w_hbm = gate_W.rearrange("(t p) o -> p t o", p=P)
+    dw_hbm = out_1.rearrange("(t p) o -> p t o", p=P)
 
     with ExitStack() as ctx:
         keep = ctx.enter_context(tc.tile_pool(name="keep", bufs=1))
-        lace = ctx.enter_context(tc.tile_pool(name="lace", bufs=3))
-        grpp = ctx.enter_context(tc.tile_pool(name="grpp", bufs=3))
-        tps = ctx.enter_context(tc.psum_pool(name="tps", bufs=2))
-        ps0 = ctx.enter_context(tc.psum_pool(name="ps0", bufs=2))
-        ps1 = ctx.enter_context(tc.psum_pool(name="ps1", bufs=4))
+        laced_pool = ctx.enter_context(tc.tile_pool(name="laced_pool", bufs=3))
+        turned_pool = ctx.enter_context(tc.tile_pool(name="turned_pool", bufs=3))
+        turn_psum = ctx.enter_context(tc.psum_pool(name="turn_psum", bufs=2))
+        dx_psum = ctx.enter_context(tc.psum_pool(name="dx_psum", bufs=2))
+        dw_psum = ctx.enter_context(tc.psum_pool(name="dw_psum", bufs=4))
 
-        ident = keep.tile([P, P], F32, name="ident")
-        make_identity(nc, ident[:])
-        neg_half = keep.tile([P, 1], F32, name="neg_half")
-        nc.vector.memset(neg_half[:], -0.5)
-        warm = keep.tile([P, 1], F32, name="warm")
-        nc.scalar.activation(out=warm[:], in_=neg_half[:], func=ACT.Sigmoid)
+        identity = keep.tile([P, P], F32, name="identity")
+        make_identity(nc, identity[:])
+        minus_half = keep.tile([P, 1], F32, name="minus_half")
+        nc.vector.memset(minus_half[:], -0.5)
+        table_warmer = keep.tile([P, 1], F32, name="table_warmer")
+        nc.scalar.activation(out=table_warmer[:], in_=minus_half[:], func=ACT.Sigmoid)
 
-        wraw = keep.tile([P, D // P, D], BF16, name="wraw")
-        wT_c = [keep.tile([P, D], U32, name="wT_c%d" % h, align_bytes=64) for h in range(NH)]
-        wT_s = [keep.tile([P, D], U8, name="wT_s%d" % h, align_bytes=64) for h in range(NH)]
-        x_c = [keep.tile([P, D], U32, name="x_c%d" % g, align_bytes=64) for g in range(NG)]
-        x_s = [keep.tile([P, D], U8, name="x_s%d" % g, align_bytes=64) for g in range(NG)]
-        d1_c = [[keep.tile([P, KP], U32, name="d1_c%d_%d" % (g, h), align_bytes=64) for h in range(NH)] for g in range(NG)]
-        d1_s = [[keep.tile([P, KP], U8, name="d1_s%d_%d" % (g, h), align_bytes=64) for h in range(NH)] for g in range(NG)]
-        dT_c = [[[keep.tile([P, 2 * P], U32, name="dT_c%d_%d_%d" % (g, a, h), align_bytes=64) for h in range(NH)] for a in range(2)] for g in range(NG)]
-        dT_s = [[[keep.tile([P, 2 * P], U8, name="dT_s%d_%d_%d" % (g, a, h), align_bytes=64) for h in range(NH)] for a in range(2)] for g in range(NG)]
-        zt = [keep.tile([P, nj, nw], F32, name="zt%d" % r) for r, (g, j0, nj, w0, nw) in enumerate(RECTS)]
-        ft = [keep.tile([P, nj, nw], F32, name="ft%d" % r) for r, (g, j0, nj, w0, nw) in enumerate(RECTS)]
-        gt = [keep.tile([P, PACK, D], BF16, name="gt%d" % g) for g in range(NG)]
-        xt = [keep.tile([P, PACK, D], BF16, name="xt%d" % g) for g in range(NG)]
+        w_raw = keep.tile([P, W_TILES, FEATURES], BF16, name="w_raw")
+        z_sb = [keep.tile([P, nj, nw], F32, name="z_sb%d" % panel) for panel, (g, j0, nj, w0, nw) in enumerate(PANELS)]
+        flow_sb = [keep.tile([P, nj, nw], F32, name="flow_sb%d" % panel) for panel, (g, j0, nj, w0, nw) in enumerate(PANELS)]
+        dz_sb = [keep.tile([P, PACK, FEATURES], BF16, name="dz_sb%d" % g) for g in range(GROUPS)]
+        x_sb = [keep.tile([P, PACK, FEATURES], BF16, name="x_sb%d" % g) for g in range(GROUPS)]
 
-        o0t = {}
+        def code_tile(name, width):
+            return keep.tile([P, width], U32, name=name, align_bytes=64)
+
+        def scale_tile(name, width):
+            return keep.tile([P, width], U8, name=name, align_bytes=64)
+
+        w_codes = [code_tile("w_codes%d" % h, FEATURES) for h in range(HALVES)]
+        w_scales = [scale_tile("w_scales%d" % h, FEATURES) for h in range(HALVES)]
+        x_codes = [code_tile("x_codes%d" % g, FEATURES) for g in range(GROUPS)]
+        x_scales = [scale_tile("x_scales%d" % g, FEATURES) for g in range(GROUPS)]
+        dzk_tok_codes = [[code_tile("dzk_tok_codes%d_%d" % (g, h), HALF) for h in range(HALVES)] for g in range(GROUPS)]
+        dzk_tok_scales = [[scale_tile("dzk_tok_scales%d_%d" % (g, h), HALF) for h in range(HALVES)] for g in range(GROUPS)]
+        dzk_feat_codes = [
+            [[code_tile("dzk_feat_codes%d_%d_%d" % (g, a, h), 2 * P) for h in range(HALVES)] for a in range(2)]
+            for g in range(GROUPS)
+        ]
+        dzk_feat_scales = [
+            [[scale_tile("dzk_feat_scales%d_%d_%d" % (g, a, h), 2 * P) for h in range(HALVES)] for a in range(2)]
+            for g in range(GROUPS)
+        ]
+
+        dx_stage = {}
         for g in range(2):
             for a in range(2):
-                o0t[(g, a)] = ft[2 * g + a][:]
-        o0t[(2, 0)] = ft[4][:].rearrange("p a b -> p (a b)").rearrange("p (i c) -> p i c", i=2)
-        o0t[(2, 1)] = zt[4][:].rearrange("p a b -> p (a b)").rearrange("p (i c) -> p i c", i=2)
-        o1t = {}
-        for h in range(NH):
-            for ip in range(4):
-                o1t[(ip, h)] = zt[2 * h + ip // 2][:, ip % 2, :].rearrange("p (i c) -> p i c", i=2)
+                dx_stage[(g, a)] = flow_sb[2 * g + a][:]
+        dx_stage[(2, 0)] = flow_sb[4][:].rearrange("p j w -> p (j w)").rearrange("p (i c) -> p i c", i=2)
+        dx_stage[(2, 1)] = z_sb[4][:].rearrange("p j w -> p (j w)").rearrange("p (i c) -> p i c", i=2)
+        dw_stage = {}
+        for h in range(HALVES):
+            for q in range(W_TILES // 2):
+                dw_stage[(q, h)] = z_sb[2 * h + q // 2][:, q % 2, :].rearrange("p (i c) -> p i c", i=2)
 
-        bank = {}
-        grp = {}
+        turn_bank = {}
+        turned = {}
         laced = {}
-        acc0 = {}
-        acc1 = {}
+        dx_acc = {}
+        dw_acc = {}
 
-        def pieces(r):
-            g, j0, nj, w0, nw = RECTS[r]
-            step = PIECE // nw
-            return [(js, step) for js in range(0, nj, step)]
 
-        def load_rect(tiles, view, r, split):
-            g, j0, nj, w0, nw = RECTS[r]
-            cuts = pieces(r) if split else [(0, nj)]
-            for js, step in cuts:
-                nc.sync.dma_start(
-                    out=tiles[r][:, js : js + step, :], in_=view[:, g, j0 + js : j0 + js + step, w0 : w0 + nw]
-                )
+        def load_part(tiles, hbm, panel, js, nj, ws, nw):
+            g, j0, w0 = PANELS[panel][0], PANELS[panel][1], PANELS[panel][3]
+            nc.sync.dma_start(
+                out=tiles[panel][:, js : js + nj, ws : ws + nw],
+                in_=hbm[:, g, j0 + js : j0 + js + nj, w0 + ws : w0 + ws + nw],
+            )
 
-        def load_z(r, split):
-            load_rect(zt, zv, r, split)
+        def load_piece(tiles, hbm, panel, piece):
+            js, nj, ws, nw = PIECES[panel][piece]
+            load_part(tiles, hbm, panel, js, nj, ws, nw)
 
-        def load_f(r, split):
-            load_rect(ft, fv, r, split)
+        def load_panel(tiles, hbm, panel):
+            load_part(tiles, hbm, panel, 0, PANELS[panel][2], 0, PANELS[panel][4])
 
-        def load_g(g, a):
-            nc.sync.dma_start(out=gt[g][:, 2 * a : 2 * a + 2, :], in_=gv[:, g, 2 * a : 2 * a + 2, :])
+        def load_grad(g, a):
+            nc.sync.dma_start(out=dz_sb[g][:, 2 * a : 2 * a + 2, :], in_=grad_hbm[:, g, 2 * a : 2 * a + 2, :])
 
         def load_x(g):
-            nc.sync.dma_start(out=xt[g][:], in_=xv[:, g, :, :])
+            nc.sync.dma_start(out=x_sb[g][:], in_=x_hbm[:, g, :, :])
 
-        def load_w(a0):
-            nc.sync.dma_start(out=wraw[:, a0 : a0 + 2, :], in_=wv[:, a0 : a0 + 2, :])
+        def load_w(t):
+            nc.sync.dma_start(out=w_raw[:, t : t + 2, :], in_=w_hbm[:, t : t + 2, :])
 
-        def zpiece(r, p):
-            js, step = pieces(r)[p]
-            return zt[r][:, js : js + step, :]
 
-        def sig(r, p):
-            v = zpiece(r, p)
-            nc.scalar.activation(out=v, in_=v, func=ACT.Sigmoid)
+        def z_piece(panel, piece):
+            js, nj, ws, nw = PIECES[panel][piece]
+            return z_sb[panel][:, js : js + nj, ws : ws + nw]
 
-        def sq(r, p):
-            v = zpiece(r, p)
-            nc.scalar.activation(out=v, in_=v, func=ACT.Square, bias=neg_half[:])
+        def sigmoid(panel, piece):
+            nc.scalar.activation(out=z_piece(panel, piece), in_=z_piece(panel, piece), func=ACT.Sigmoid)
 
-        def C(r, p):
-            js, step = pieces(r)[p]
-            v = zpiece(r, p)
+        def square(panel, piece):
+            nc.scalar.activation(out=z_piece(panel, piece), in_=z_piece(panel, piece), func=ACT.Square, bias=minus_half[:])
+
+        def times_flow(panel, piece):
+            js, nj, ws, nw = PIECES[panel][piece]
             nc.vector.scalar_tensor_tensor(
-                out=v, in0=v, scalar=0.25, in1=ft[r][:, js : js + step, :], op0=ALU.subtract, op1=ALU.mult
+                out=z_piece(panel, piece),
+                in0=z_piece(panel, piece),
+                scalar=0.25,
+                in1=flow_sb[panel][:, js : js + nj, ws : ws + nw],
+                op0=ALU.subtract,
+                op1=ALU.mult,
             )
 
-        def Dz(r, p):
-            g, j0, nj, w0, nw = RECTS[r]
-            js, step = pieces(r)[p]
-            spot = gt[g][:, j0 + js : j0 + js + step, w0 : w0 + nw]
+        def times_grad(panel, piece):
+            g, j0, w0 = PANELS[panel][0], PANELS[panel][1], PANELS[panel][3]
+            js, nj, ws, nw = PIECES[panel][piece]
+            spot = dz_sb[g][:, j0 + js : j0 + js + nj, w0 + ws : w0 + ws + nw]
             nc.vector.scalar_tensor_tensor(
-                out=spot, in0=zpiece(r, p), scalar=-1.0, in1=spot, op0=ALU.mult, op1=ALU.mult
+                out=spot, in0=z_piece(panel, piece), scalar=-1.0, in1=spot, op0=ALU.mult, op1=ALU.mult
             )
 
-        def copy_on(eng, out, in_):
-            if eng == "S":
-                nc.scalar.copy(out=out, in_=in_)
-            else:
-                nc.vector.tensor_copy(out=out, in_=in_)
 
-        def turn_T(key, words, rows, h):
-            bank[key] = tps.tile([P, 2, 2, P], F32, name="bank", tag="bank")
+        def turn(key, words, first, h):
+            turn_bank[key] = turn_psum.tile([P, 2, 2, P], F32, name="turn_bank", tag="turn_bank")
             for i in range(2):
                 for u in range(2):
                     nc.tensor.transpose(
-                        bank[key][:, i, u, :], words[:, rows[i], 256 * h + u : 256 * (h + 1) : 2], ident[:]
+                        turn_bank[key][:, i, u, :], words[:, first + i, WORDS * h + u : WORDS * (h + 1) : 2], identity[:]
                     )
 
-        def turn_C(key, eng):
-            grp[key] = grpp.tile([P, 2, P, PACK], BF16, name="grp", tag="grp", align_bytes=64)
-            copy_on(eng, grp[key][:].bitcast(F32), bank[key][:].rearrange("m i u r -> m i r u"))
+        def copy_turned(key):
+            turned[key] = turned_pool.tile([P, 2, P, PACK], BF16, name="turned", tag="turned", align_bytes=64)
+            nc.scalar.copy(out=turned[key][:].bitcast(F32), in_=turn_bank[key][:].rearrange("m i u r -> m i r u"))
 
-        def turn_Q(key, codes, scales, fmt):
+        def quantize_turned(key, code_words, scale_bytes, fmt):
             nc.vector.quantize_mx(
-                out=codes.bitcast(fmt), scales=scales, in_=grp[key][:].rearrange("m i r t -> m (i r t)")
+                out=code_words.bitcast(fmt), scales=scale_bytes, in_=turned[key][:].rearrange("m i r v -> m (i r v)")
             )
 
-        def wT(h, ip):
-            turn_T(("w", h, ip), wraw[:].bitcast(F32), (2 * ip, 2 * ip + 1), h)
+        def turn_w(h, q):
+            turn(("w", h, q), w_raw[:].bitcast(F32), 2 * q, h)
 
-        def wC(h, ip, eng):
-            turn_C(("w", h, ip), eng)
+        def copy_w(h, q):
+            copy_turned(("w", h, q))
 
-        def wQ(h, ip):
-            cols = slice(2 * P * ip, 2 * P * (ip + 1))
-            turn_Q(("w", h, ip), wT_c[h][:, cols], wT_s[h][:, cols], E4M3)
+        def quantize_w(h, q):
+            cols = slice(2 * P * q, 2 * P * (q + 1))
+            quantize_turned(("w", h, q), w_codes[h][:, cols], w_scales[h][:, cols], E4M3)
 
-        def dT(g, a, h):
-            turn_T((g, a, h), gt[g][:].bitcast(F32), (2 * a, 2 * a + 1), h)
+        def turn_dz(g, a, h):
+            turn((g, a, h), dz_sb[g][:].bitcast(F32), 2 * a, h)
 
-        def dC(g, a, h, eng):
-            turn_C((g, a, h), eng)
+        def copy_dz(g, a, h):
+            copy_turned((g, a, h))
 
-        def dQ(g, a, h):
-            turn_Q((g, a, h), dT_c[g][a][h][:], dT_s[g][a][h][:], E5M2)
+        def quantize_dz(g, a, h):
+            quantize_turned((g, a, h), dzk_feat_codes[g][a][h][:], dzk_feat_scales[g][a][h][:], E5M2)
 
-        def lace_copy(key, src, eng):
-            laced[key] = lace.tile([P, KP, PACK], BF16, name="laced", tag="laced", align_bytes=64)
-            copy_on(
-                eng,
-                laced[key][:].rearrange("p (c i) t -> p c t i", i=4),
-                src.rearrange("p t (c i) -> p c t i", i=4),
+
+        def lace(key, by_slot):
+            laced[key] = laced_pool.tile([P, HALF, PACK], BF16, name="laced", tag="laced", align_bytes=64)
+            nc.vector.tensor_copy(
+                out=laced[key][:].rearrange("p (d f) j -> p d j f", f=RUN),
+                in_=by_slot.rearrange("p j (d f) -> p d j f", f=RUN),
             )
 
-        def lace_quant(key, codes, scales, fmt):
+        def quantize_laced(key, code_words, scale_bytes, fmt):
             nc.vector.quantize_mx(
-                out=codes.bitcast(fmt), scales=scales, in_=laced[key][:].rearrange("p w t -> p (w t)")
+                out=code_words.bitcast(fmt), scales=scale_bytes, in_=laced[key][:].rearrange("p w j -> p (w j)")
             )
 
-        def lD(g, h):
-            lace_copy(("d", g, h), gt[g][:, :, KP * h : KP * (h + 1)], "V")
+        def lace_x(g, h):
+            lace(("x", g, h), x_sb[g][:, :, HALF * h : HALF * (h + 1)])
 
-        def qD(g, h):
-            lace_quant(("d", g, h), d1_c[g][h][:], d1_s[g][h][:], E5M2)
+        def quantize_x(g, h):
+            cols = slice(HALF * h, HALF * (h + 1))
+            quantize_laced(("x", g, h), x_codes[g][:, cols], x_scales[g][:, cols], E4M3)
 
-        def lX(g, h, eng):
-            lace_copy(("x", g, h), xt[g][:, :, KP * h : KP * (h + 1)], eng)
+        def lace_dz(g, h):
+            lace(("dz", g, h), dz_sb[g][:, :, HALF * h : HALF * (h + 1)])
 
-        def qX(g, h):
-            cols = slice(KP * h, KP * (h + 1))
-            lace_quant(("x", g, h), x_c[g][:, cols], x_s[g][:, cols], E4M3)
+        def quantize_laced_dz(g, h):
+            quantize_laced(("dz", g, h), dzk_tok_codes[g][h][:], dzk_tok_scales[g][h][:], E5M2)
 
-        def mm0(g, a, i, n, h):
+
+        def drain(out, acc, on_vector):
+            if on_vector:
+                nc.vector.tensor_copy(out=out, in_=acc)
+            else:
+                nc.scalar.copy(out=out, in_=acc)
+
+        def mm_dx(g, a, i, n, h):
             if h == 0:
-                acc0[(g, a, i, n)] = ps0.tile([P, KP], F32, name="acc0", tag="acc0")
-            rows = slice(P * i, P * (i + 1))
-            cols = slice(KP * n, KP * (n + 1))
+                dx_acc[(g, a, i, n)] = dx_psum.tile([P, HALF], F32, name="dx_acc", tag="dx_acc")
+            tokens = slice(P * i, P * (i + 1))
+            cols = slice(HALF * n, HALF * (n + 1))
             nc.tensor.matmul_mx(
-                out=acc0[(g, a, i, n)][:],
-                lhsT=dT_c[g][a][h][:, rows].bitcast(E5M2),
-                lhsT_scale=dT_s[g][a][h][:, rows],
-                rhs=wT_c[h][:, cols].bitcast(E4M3),
-                rhs_scale=wT_s[h][:, cols],
+                out=dx_acc[(g, a, i, n)][:],
+                lhsT=dzk_feat_codes[g][a][h][:, tokens].bitcast(E5M2),
+                lhsT_scale=dzk_feat_scales[g][a][h][:, tokens],
+                rhs=w_codes[h][:, cols].bitcast(E4M3),
+                rhs_scale=w_scales[h][:, cols],
                 start=(h == 0),
-                stop=(h == NH - 1),
+                stop=(h == HALVES - 1),
             )
 
-        def ev0(g, a, i, n, eng):
-            copy_on(eng, o0t[(g, a)][:, i, KP * n : KP * (n + 1)], acc0[(g, a, i, n)][:])
+        def mm_dx_pass(g, a, i, h):
+            for n in range(HALVES):
+                mm_dx(g, a, i, n, h)
 
-        def s0(g, a):
-            nc.sync.dma_start(out=o0v[:, g, 2 * a : 2 * a + 2, :], in_=o0t[(g, a)])
+        def mm_dx_whole(g, a, i):
+            for n in range(HALVES):
+                for h in range(HALVES):
+                    mm_dx(g, a, i, n, h)
 
-        def mm1(ia, h, g):
+        def drain_dx(g, a, i, share):
+            for n in range(HALVES):
+                drain(dx_stage[(g, a)][:, i, HALF * n : HALF * (n + 1)], dx_acc[(g, a, i, n)][:], share and n == 1)
+
+        def store_dx(g, a):
+            nc.sync.dma_start(out=dx_hbm[:, g, 2 * a : 2 * a + 2, :], in_=dx_stage[(g, a)])
+
+        def store_dx_slot(g, a, i):
+            nc.sync.dma_start(out=dx_hbm[:, g, 2 * a + i, :], in_=dx_stage[(g, a)][:, i, :])
+
+        def mm_dw(t, h, g):
             if g == 0:
-                acc1[(ia, h)] = ps1.tile([P, KP], F32, name="acc1", tag="acc1")
-            rows = slice(P * ia, P * (ia + 1))
+                dw_acc[(t, h)] = dw_psum.tile([P, HALF], F32, name="dw_acc", tag="dw_acc")
+            cols = slice(P * t, P * (t + 1))
             nc.tensor.matmul_mx(
-                out=acc1[(ia, h)][:],
-                lhsT=x_c[g][:, rows].bitcast(E4M3),
-                lhsT_scale=x_s[g][:, rows],
-                rhs=d1_c[g][h][:].bitcast(E5M2),
-                rhs_scale=d1_s[g][h][:],
+                out=dw_acc[(t, h)][:],
+                lhsT=x_codes[g][:, cols].bitcast(E4M3),
+                lhsT_scale=x_scales[g][:, cols],
+                rhs=dzk_tok_codes[g][h][:].bitcast(E5M2),
+                rhs_scale=dzk_tok_scales[g][h][:],
                 start=(g == 0),
-                stop=(g == NG - 1),
+                stop=(g == GROUPS - 1),
             )
 
-        def ev1(ia, h, eng):
-            copy_on(eng, o1t[(ia // 2, h)][:, ia % 2, :], acc1[(ia, h)][:])
+        def drain_dw(t, h, on_vector):
+            drain(dw_stage[(t // 2, h)][:, t % 2, :], dw_acc[(t, h)][:], on_vector)
 
-        def s1(ip, h):
-            nc.sync.dma_start(out=o1v[:, 2 * ip : 2 * ip + 2, KP * h : KP * (h + 1)], in_=o1t[(ip, h)])
+        def store_dw_pair(q, h):
+            nc.sync.dma_start(out=dw_hbm[:, 2 * q : 2 * q + 2, HALF * h : HALF * (h + 1)], in_=dw_stage[(q, h)])
+
+        def store_dw(t, h):
+            nc.sync.dma_start(out=dw_hbm[:, t, HALF * h : HALF * (h + 1)], in_=dw_stage[(t // 2, h)][:, t % 2, :])
+
+        held = range(W_TILES // 2)
+        late = range(W_TILES // 2, W_TILES)
 
         with tc.manual_schedule():
-            load_z(0, True)
-            load_f(0, True)
-            sig(0, 0)
-            sig(0, 1)
-            load_g(0, 0)
-            sq(0, 0)
-            load_w(0)
-            sq(0, 1)
-            C(0, 0)
-            load_w(2)
-            C(0, 1)
-            load_w(4)
-            Dz(0, 0)
-            wT(0, 0)
-            wT(1, 0)
-            wC(0, 0, "S")
-            load_w(6)
-            Dz(0, 1)
-            wC(1, 0, "S")
-            wT(0, 1)
-            wT(1, 1)
-            wC(0, 1, "S")
+            load_piece(z_sb, z_hbm, 0, 0)
+            load_piece(flow_sb, flow_hbm, 0, 0)
+            load_grad(0, 0)
             load_x(0)
-            wQ(0, 0)
-            wQ(1, 0)
-            wC(1, 1, "S")
-            wT(0, 2)
-            wQ(0, 1)
-            wC(0, 2, "S")
-            wQ(1, 1)
-            wT(1, 2)
-            wC(1, 2, "S")
-            wQ(0, 2)
-            wT(0, 3)
-            load_z(1, False)
-            wC(0, 3, "S")
-            wQ(1, 2)
-            wT(1, 3)
-            wC(1, 3, "S")
-            wQ(0, 3)
-            dT(0, 0, 0)
-            dC(0, 0, 0, "S")
-            wQ(1, 3)
-            dT(0, 0, 1)
-            lX(0, 0, "V")
-            dC(0, 0, 1, "S")
-            load_f(1, False)
-            lX(0, 1, "V")
-            sig(1, 0)
-            load_g(0, 1)
-            qX(0, 0)
-            sig(1, 1)
-            dQ(0, 0, 0)
-            qX(0, 1)
-            load_z(2, False)
-            mm0(0, 0, 0, 0, 0)
-            mm0(0, 0, 0, 1, 0)
-            dQ(0, 0, 1)
-            sq(1, 0)
-            mm0(0, 0, 0, 0, 1)
-            mm0(0, 0, 0, 1, 1)
-            sq(1, 1)
-            C(1, 0)
-            load_f(2, False)
-            ev0(0, 0, 0, 0, "S")
-            C(1, 1)
-            ev0(0, 0, 0, 1, "S")
-            mm0(0, 0, 1, 0, 0)
-            mm0(0, 0, 1, 0, 1)
-            sig(2, 0)
-            Dz(1, 0)
-            mm0(0, 0, 1, 1, 0)
-            mm0(0, 0, 1, 1, 1)
-            load_g(1, 0)
-            ev0(0, 0, 1, 0, "S")
-            Dz(1, 1)
-            load_x(1)
-            ev0(0, 0, 1, 1, "S")
-            sq(2, 0)
-            lD(0, 0)
-            dT(0, 1, 0)
-            dT(0, 1, 1)
-            sig(2, 1)
-            load_z(3, False)
-            C(2, 0)
-            dC(0, 1, 0, "S")
-            qD(0, 0)
-            sq(2, 1)
-            dQ(0, 1, 0)
-            mm1(0, 0, 0)
-            lX(1, 0, "V")
-            load_f(3, False)
-            mm0(0, 1, 0, 0, 0)
-            dC(0, 1, 1, "S")
-            mm0(0, 1, 0, 1, 0)
-            mm1(1, 0, 0)
-            mm1(2, 0, 0)
-            mm1(3, 0, 0)
-            lX(1, 1, "V")
-            sig(3, 0)
-            load_g(1, 1)
-            qX(1, 0)
-            sig(3, 1)
-            qX(1, 1)
-            load_z(4, False)
-            dQ(0, 1, 1)
-            Dz(2, 0)
-            sq(3, 0)
-            mm0(0, 1, 0, 0, 1)
-            mm0(0, 1, 0, 1, 1)
-            C(2, 1)
-            ev0(0, 1, 0, 0, "S")
-            ev0(0, 1, 0, 1, "S")
-            mm0(0, 1, 1, 0, 0)
-            load_f(4, False)
-            mm0(0, 1, 1, 0, 1)
-            C(3, 0)
-            sq(3, 1)
-            mm0(0, 1, 1, 1, 0)
-            mm0(0, 1, 1, 1, 1)
-            Dz(2, 1)
-            ev0(0, 1, 1, 0, "S")
-            ev0(0, 1, 1, 1, "S")
-            load_g(2, 0)
-            Dz(3, 0)
-            sig(4, 0)
-            dT(1, 0, 0)
-            dT(1, 0, 1)
-            load_g(2, 1)
-            C(3, 1)
-            dC(1, 0, 0, "S")
-            dC(1, 0, 1, "S")
+            for piece in (1, 2):
+                load_piece(z_sb, z_hbm, 0, piece)
+                load_piece(flow_sb, flow_hbm, 0, piece)
+            load_panel(z_sb, z_hbm, 1)
+            load_panel(flow_sb, flow_hbm, 1)
+            load_grad(0, 1)
+            for t in range(0, W_TILES, 2):
+                load_w(t)
+            for a in range(2):
+                load_panel(z_sb, z_hbm, 2 + a)
+                load_panel(flow_sb, flow_hbm, 2 + a)
+                load_grad(1, a)
+                if a == 0:
+                    load_x(1)
+            load_panel(z_sb, z_hbm, 4)
+            load_panel(flow_sb, flow_hbm, 4)
+            load_grad(2, 0)
+            load_grad(2, 1)
             load_x(2)
-            dQ(1, 0, 0)
-            sq(4, 0)
-            dQ(1, 0, 1)
-            mm0(1, 0, 0, 0, 0)
-            Dz(3, 1)
-            mm0(1, 0, 0, 0, 1)
-            mm0(1, 0, 0, 1, 0)
-            sig(4, 1)
-            mm0(1, 0, 0, 1, 1)
-            C(4, 0)
-            dT(1, 1, 0)
-            load_z(5, False)
-            ev0(1, 0, 0, 0, "S")
-            dT(1, 1, 1)
-            ev0(1, 0, 0, 1, "S")
-            lD(1, 0)
-            mm0(1, 0, 1, 0, 0)
-            mm0(1, 0, 1, 0, 1)
-            sq(4, 1)
-            load_f(5, False)
-            mm0(1, 0, 1, 1, 0)
-            mm0(1, 0, 1, 1, 1)
-            lX(2, 0, "V")
-            ev0(1, 0, 1, 0, "S")
-            load_z(6, False)
-            ev0(1, 0, 1, 1, "S")
-            lX(2, 1, "V")
-            dC(1, 1, 0, "S")
-            load_f(6, False)
-            dC(1, 1, 1, "S")
-            sig(5, 0)
-            qX(2, 0)
-            s0(0, 0)
-            qX(2, 1)
-            sig(6, 0)
-            dQ(1, 1, 0)
-            dQ(1, 1, 1)
-            mm0(1, 1, 0, 0, 0)
-            Dz(4, 0)
-            mm0(1, 1, 0, 0, 1)
-            sq(5, 0)
-            mm0(1, 1, 0, 1, 0)
-            mm0(1, 1, 0, 1, 1)
-            s0(0, 1)
-            qD(1, 0)
-            dT(2, 0, 0)
-            ev0(1, 1, 0, 0, "S")
-            C(4, 1)
-            ev0(1, 1, 0, 1, "S")
-            mm1(0, 0, 1)
-            mm0(1, 1, 1, 0, 0)
-            dC(2, 0, 0, "S")
-            mm0(1, 1, 1, 0, 1)
-            C(5, 0)
-            mm0(1, 1, 1, 1, 0)
-            ev0(1, 1, 1, 0, "S")
-            s0(1, 0)
-            mm0(1, 1, 1, 1, 1)
-            mm1(1, 0, 1)
-            ev0(1, 1, 1, 1, "S")
-            mm1(2, 0, 1)
-            dQ(2, 0, 0)
-            mm1(3, 0, 1)
-            sq(6, 0)
-            Dz(4, 1)
-            mm0(2, 0, 0, 0, 0)
-            mm0(2, 0, 0, 1, 0)
-            s0(1, 1)
-            Dz(5, 0)
-            dT(2, 1, 0)
-            dC(2, 1, 0, "S")
-            lD(2, 0)
-            dT(2, 0, 1)
-            dC(2, 0, 1, "S")
-            dQ(2, 1, 0)
-            qD(2, 0)
-            lD(0, 1)
-            mm1(0, 0, 2)
-            mm1(1, 0, 2)
-            ev1(0, 0, "S")
-            mm1(2, 0, 2)
-            mm1(3, 0, 2)
-            ev1(1, 0, "S")
-            lD(1, 1)
-            mm1(4, 0, 0)
-            mm1(4, 0, 1)
-            ev1(2, 0, "S")
-            s1(0, 0)
-            mm1(4, 0, 2)
-            mm1(5, 0, 0)
-            ev1(3, 0, "S")
-            mm1(5, 0, 1)
-            dQ(2, 0, 1)
-            mm1(5, 0, 2)
-            ev1(4, 0, "S")
-            qD(0, 1)
-            mm1(6, 0, 0)
-            s1(1, 0)
-            mm1(6, 0, 1)
-            ev1(5, 0, "S")
-            qD(1, 1)
-            mm1(6, 0, 2)
-            mm1(7, 0, 0)
-            ev1(6, 0, "S")
-            mm1(7, 0, 1)
-            C(6, 0)
-            s1(2, 0)
-            mm1(7, 0, 2)
-            mm1(0, 1, 0)
-            ev1(7, 0, "S")
-            mm1(1, 1, 0)
-            mm1(2, 1, 0)
-            Dz(6, 0)
-            mm1(3, 1, 0)
-            s1(3, 0)
-            mm1(0, 1, 1)
-            mm1(1, 1, 1)
-            mm1(2, 1, 1)
-            mm1(3, 1, 1)
-            lD(2, 1)
-            mm0(2, 0, 0, 0, 1)
-            mm0(2, 0, 0, 1, 1)
-            ev0(2, 0, 0, 0, "S")
-            dT(2, 1, 1)
-            ev0(2, 0, 0, 1, "V")
-            mm0(2, 0, 1, 0, 0)
-            mm0(2, 0, 1, 0, 1)
-            qD(2, 1)
-            ev0(2, 0, 1, 0, "S")
-            mm0(2, 0, 1, 1, 0)
-            dC(2, 1, 1, "S")
-            mm0(2, 0, 1, 1, 1)
-            mm1(0, 1, 2)
-            ev0(2, 0, 1, 1, "V")
-            mm1(1, 1, 2)
-            ev1(0, 1, "S")
-            mm1(2, 1, 2)
-            dQ(2, 1, 1)
-            s0(2, 0)
-            mm1(3, 1, 2)
-            ev1(2, 1, "S")
-            ev1(1, 1, "V")
-            mm1(4, 1, 0)
-            mm1(4, 1, 1)
-            ev1(3, 1, "V")
-            mm1(4, 1, 2)
-            mm1(5, 1, 0)
-            ev1(4, 1, "S")
-            mm1(5, 1, 1)
-            mm1(5, 1, 2)
-            mm1(6, 1, 0)
-            ev1(5, 1, "V")
-            s1(0, 1)
-            mm1(6, 1, 1)
-            mm1(6, 1, 2)
-            mm1(7, 1, 0)
-            ev1(6, 1, "S")
-            mm1(7, 1, 1)
-            mm1(7, 1, 2)
-            s1(1, 1)
-            mm0(2, 1, 0, 0, 0)
-            ev1(7, 1, "V")
-            mm0(2, 1, 0, 0, 1)
-            mm0(2, 1, 0, 1, 0)
-            ev0(2, 1, 0, 0, "S")
-            mm0(2, 1, 0, 1, 1)
-            s1(2, 1)
-            ev0(2, 1, 0, 1, "V")
-            mm0(2, 1, 1, 0, 0)
-            mm0(2, 1, 1, 0, 1)
-            mm0(2, 1, 1, 1, 0)
-            ev0(2, 1, 1, 0, "S")
-            mm0(2, 1, 1, 1, 1)
-            s1(3, 1)
-            ev0(2, 1, 1, 1, "V")
-            s0(2, 1)
+            for panel in (5, 6):
+                load_panel(z_sb, z_hbm, panel)
+                load_panel(flow_sb, flow_hbm, panel)
+
+            for piece in range(3):
+                sigmoid(0, piece)
+                square(0, piece)
+            times_flow(0, 0)
+            times_grad(0, 0)
+            lace_x(0, 1)
+            lace_x(0, 0)
+            times_flow(0, 1)
+            quantize_x(0, 1)
+            times_grad(0, 1)
+            quantize_x(0, 0)
+            times_flow(0, 2)
+            times_grad(0, 2)
+
+            sigmoid(1, 0)
+            sigmoid(1, 1)
+            square(1, 0)
+            square(1, 1)
+            times_flow(1, 0)
+            times_flow(1, 1)
+            times_grad(1, 0)
+            for q in range(W_TILES // 2):
+                for h in range(HALVES):
+                    turn_w(h, q)
+                    copy_w(h, q)
+                    quantize_w(h, q)
+                    if (q, h) == (0, 1):
+                        times_grad(1, 1)
+                    if (q, h) == (2, 0):
+                        lace_dz(0, 1)
+            quantize_laced_dz(0, 1)
+            lace_dz(0, 0)
+
+            turn_dz(0, 0, 0)
+            turn_dz(0, 0, 1)
+            sigmoid(2, 0)
+            copy_dz(0, 0, 0)
+            square(2, 0)
+            copy_dz(0, 0, 1)
+            sigmoid(2, 1)
+            turn_dz(0, 1, 0)
+            quantize_dz(0, 0, 0)
+            quantize_laced_dz(0, 0)
+            quantize_dz(0, 0, 1)
+            mm_dx_pass(0, 0, 0, 0)
+            turn_dz(0, 1, 1)
+            mm_dx_pass(0, 0, 0, 1)
+            drain_dx(0, 0, 0, False)
+            square(2, 1)
+            mm_dx_whole(0, 0, 1)
+            drain_dx(0, 0, 1, False)
+            for t in held:
+                mm_dw(t, 0, 0)
+
+            times_flow(2, 0)
+            times_grad(2, 0)
+            lace_x(1, 0)
+            times_flow(2, 1)
+            quantize_x(1, 0)
+            copy_dz(0, 1, 0)
+            sigmoid(3, 0)
+            copy_dz(0, 1, 1)
+            square(3, 0)
+            sigmoid(3, 1)
+            quantize_dz(0, 1, 0)
+            times_grad(2, 1)
+            quantize_dz(0, 1, 1)
+            lace_x(1, 1)
+            mm_dx_pass(0, 1, 0, 0)
+            turn_dz(1, 0, 0)
+            mm_dx_pass(0, 1, 0, 1)
+            turn_dz(1, 0, 1)
+            drain_dx(0, 1, 0, False)
+            square(3, 1)
+            mm_dx_whole(0, 1, 1)
+            drain_dx(0, 1, 1, False)
+
+            times_flow(3, 0)
+            quantize_x(1, 1)
+            times_grad(3, 0)
+            times_flow(3, 1)
+            times_grad(3, 1)
+            sigmoid(4, 0)
+            copy_dz(1, 0, 0)
+            square(4, 0)
+            copy_dz(1, 0, 1)
+            sigmoid(4, 1)
+            quantize_dz(1, 0, 0)
+            lace_dz(1, 0)
+            quantize_dz(1, 0, 1)
+            turn_dz(1, 1, 0)
+            mm_dx_pass(1, 0, 0, 0)
+            turn_dz(1, 1, 1)
+            mm_dx_pass(1, 0, 0, 1)
+            copy_dz(1, 1, 0)
+            drain_dx(1, 0, 0, False)
+            square(4, 1)
+            mm_dx_whole(1, 0, 1)
+            drain_dx(1, 0, 1, False)
+
+            times_flow(4, 0)
+            quantize_laced_dz(1, 0)
+            quantize_dz(1, 1, 0)
+            times_grad(4, 0)
+            lace_x(2, 0)
+            times_flow(4, 1)
+            quantize_x(2, 0)
+            times_grad(4, 1)
+            sigmoid(5, 0)
+            copy_dz(1, 1, 1)
+            square(5, 0)
+            sigmoid(6, 0)
+            quantize_dz(1, 1, 1)
+            lace_x(2, 1)
+            lace_dz(2, 0)
+            quantize_x(2, 1)
+            quantize_laced_dz(2, 0)
+            mm_dw(0, 0, 1)
+            mm_dw(1, 0, 1)
+            turn_dz(2, 0, 0)
+            mm_dx(1, 1, 0, 0, 0)
+            mm_dw(2, 0, 1)
+            mm_dx(1, 1, 0, 1, 0)
+            mm_dw(3, 0, 1)
+            turn_dz(2, 1, 0)
+            mm_dx_pass(1, 1, 0, 1)
+            drain_dx(1, 1, 0, False)
+            square(6, 0)
+            mm_dx_whole(1, 1, 1)
+            drain_dx(1, 1, 1, False)
+            for g in range(2):
+                for a in range(2):
+                    store_dx(g, a)
+            copy_dz(2, 0, 0)
+            copy_dz(2, 1, 0)
+
+            for t in held:
+                mm_dw(t, 0, 2)
+            times_flow(5, 0)
+            quantize_dz(2, 0, 0)
+            lace_dz(1, 1)
+            quantize_dz(2, 1, 0)
+            times_grad(5, 0)
+            quantize_laced_dz(1, 1)
+            times_flow(6, 0)
+            times_grad(6, 0)
+            mm_dx_pass(2, 0, 0, 0)
+            for t in held:
+                drain_dw(t, 0, False)
+            for t in late:
+                for g in range(GROUPS):
+                    mm_dw(t, 0, g)
+            for t in late:
+                drain_dw(t, 0, False)
+            for q in range(W_TILES // 2):
+                store_dw_pair(q, 0)
+
+            turn_dz(2, 0, 1)
+            copy_dz(2, 0, 1)
+            quantize_dz(2, 0, 1)
+            lace_dz(2, 1)
+            for t in held:
+                mm_dw(t, 1, 0)
+            mm_dw(0, 1, 1)
+            mm_dx_pass(2, 0, 0, 1)
+            drain_dx(2, 0, 0, True)
+            store_dx_slot(2, 0, 0)
+            mm_dw(1, 1, 1)
+            mm_dw(2, 1, 1)
+            mm_dx(2, 0, 1, 0, 0)
+            mm_dx(2, 0, 1, 0, 1)
+            mm_dw(3, 1, 1)
+            mm_dx(2, 0, 1, 1, 0)
+            mm_dx(2, 0, 1, 1, 1)
+            quantize_laced_dz(2, 1)
+            drain_dx(2, 0, 1, True)
+            store_dx_slot(2, 0, 1)
+            turn_dz(2, 1, 1)
+            copy_dz(2, 1, 1)
+            quantize_dz(2, 1, 1)
+            for t in held:
+                mm_dw(t, 1, 2)
+            for t in held:
+                drain_dw(t, 1, t % 2 == 1)
+                store_dw(t, 1)
+            mm_dx_whole(2, 1, 0)
+            mm_dw(4, 1, 0)
+            drain_dx(2, 1, 0, True)
+            mm_dx_whole(2, 1, 1)
+            mm_dw(4, 1, 1)
+            mm_dw(4, 1, 2)
+            drain_dx(2, 1, 1, True)
+            store_dx_slot(2, 1, 0)
+            store_dx_slot(2, 1, 1)
+            for t in late[1:]:
+                for g in range(GROUPS):
+                    mm_dw(t, 1, g)
+            for t in late:
+                drain_dw(t, 1, t % 2 == 1)
+                store_dw(t, 1)

@@ -370,19 +370,19 @@ def tile_splatinformationflow_pb_v_kernel(
             square(2, 0)
             copy_dz(0, 0, 1)
             sigmoid(2, 1)
-            turn_dz(0, 1, 0)
             quantize_dz(0, 0, 0)
             quantize_laced_dz(0, 0)
             quantize_dz(0, 0, 1)
             mm_dx_pass(0, 0, 0, 0)
-            turn_dz(0, 1, 1)
             mm_dx_pass(0, 0, 0, 1)
+            turn_dz(0, 1, 0)
             drain_dx(0, 0, 0, False)
             square(2, 1)
             mm_dx_whole(0, 0, 1)
+            turn_dz(0, 1, 1)
             drain_dx(0, 0, 1, False)
-            for t in held:
-                mm_dw(t, 0, 0)
+            mm_dw(0, 0, 0)
+            mm_dw(1, 0, 0)
 
             times_flow(2, 0)
             times_grad(2, 0)
@@ -401,11 +401,13 @@ def tile_splatinformationflow_pb_v_kernel(
             mm_dx_pass(0, 1, 0, 0)
             turn_dz(1, 0, 0)
             mm_dx_pass(0, 1, 0, 1)
-            turn_dz(1, 0, 1)
             drain_dx(0, 1, 0, False)
             square(3, 1)
             mm_dx_whole(0, 1, 1)
             drain_dx(0, 1, 1, False)
+            mm_dw(2, 0, 0)
+            mm_dw(3, 0, 0)
+            turn_dz(1, 0, 1)
 
             times_flow(3, 0)
             quantize_x(1, 1)
@@ -422,7 +424,6 @@ def tile_splatinformationflow_pb_v_kernel(
             quantize_dz(1, 0, 1)
             turn_dz(1, 1, 0)
             mm_dx_pass(1, 0, 0, 0)
-            turn_dz(1, 1, 1)
             mm_dx_pass(1, 0, 0, 1)
             copy_dz(1, 1, 0)
             drain_dx(1, 0, 0, False)
@@ -432,8 +433,14 @@ def tile_splatinformationflow_pb_v_kernel(
 
             times_flow(4, 0)
             quantize_laced_dz(1, 0)
+            mm_dw(0, 0, 1)
+            turn_dz(1, 1, 1)
+            mm_dw(1, 0, 1)
             quantize_dz(1, 1, 0)
             times_grad(4, 0)
+            turn_dz(2, 0, 0)
+            mm_dx_pass(1, 1, 0, 0)
+            mm_dw(2, 0, 1)
             lace_x(2, 0)
             times_flow(4, 1)
             quantize_x(2, 0)
@@ -447,18 +454,12 @@ def tile_splatinformationflow_pb_v_kernel(
             lace_dz(2, 0)
             quantize_x(2, 1)
             quantize_laced_dz(2, 0)
-            mm_dw(0, 0, 1)
-            mm_dw(1, 0, 1)
-            turn_dz(2, 0, 0)
-            mm_dx(1, 1, 0, 0, 0)
-            mm_dw(2, 0, 1)
-            mm_dx(1, 1, 0, 1, 0)
-            mm_dw(3, 0, 1)
-            turn_dz(2, 1, 0)
             mm_dx_pass(1, 1, 0, 1)
             drain_dx(1, 1, 0, False)
             square(6, 0)
             mm_dx_whole(1, 1, 1)
+            mm_dw(3, 0, 1)
+            turn_dz(2, 1, 0)
             drain_dx(1, 1, 1, False)
             for g in range(2):
                 for a in range(2):

@@ -23,7 +23,6 @@ GROUPS = TOKENS // HALF
 HALVES = FEATURES // HALF
 WORDS = HALF // 2
 W_TILES = FEATURES // P
-RUN = 4
 
 PANELS = [
     (0, 0, 2, 0, FEATURES),
@@ -212,10 +211,7 @@ def tile_splatinformationflow_pb_v_kernel(
 
         def lace(key, by_slot):
             laced[key] = laced_pool.tile([P, HALF, PACK], BF16, name="laced", tag="laced", align_bytes=64)
-            nc.vector.tensor_copy(
-                out=laced[key][:].rearrange("p (d f) j -> p d j f", f=RUN),
-                in_=by_slot.rearrange("p j (d f) -> p d j f", f=RUN),
-            )
+            nc.vector.tensor_copy(out=laced[key][:], in_=by_slot.rearrange("p j w -> p w j"))
 
         def quantize_laced(key, code_words, scale_bytes, fmt):
             nc.vector.quantize_mx(

from contextlib import ExitStack

import concourse.mybir as mybir
from concourse.masks import make_identity

TOKENS, FEATURES = 1536, 1024
FLOPS = 2 * 2 * TOKENS * FEATURES * FEATURES
BYTES = (2 + 2 + 4 + 4 + 4) * TOKENS * FEATURES + (2 + 4) * FEATURES * FEATURES

F32 = mybir.dt.float32
BF16 = mybir.dt.bfloat16
U32 = mybir.dt.uint32
U8 = mybir.dt.uint8
E4M3 = mybir.dt.float8_e4m3fn_x4
E5M2 = mybir.dt.float8_e5m2_x4
ACT = mybir.ActivationFunctionType
ALU = mybir.AluOpType

P = 128
PACK = 4
HALF = P * PACK
GROUPS = TOKENS // HALF
HALVES = FEATURES // HALF
WORDS = HALF // 2
W_TILES = FEATURES // P

PANELS = [
    (0, 0, 2, 0, FEATURES),
    (0, 2, 2, 0, FEATURES),
    (1, 0, 2, 0, FEATURES),
    (1, 2, 2, 0, FEATURES),
    (2, 0, 4, 0, HALF),
    (2, 0, 2, HALF, HALF),
    (2, 2, 2, HALF, HALF),
]
PIECES = [
    [(0, 1, 0, HALF), (0, 1, HALF, HALF), (1, 1, 0, FEATURES)],
    [(0, 1, 0, FEATURES), (1, 1, 0, FEATURES)],
    [(0, 1, 0, FEATURES), (1, 1, 0, FEATURES)],
    [(0, 1, 0, FEATURES), (1, 1, 0, FEATURES)],
    [(0, 2, 0, HALF), (2, 2, 0, HALF)],
    [(0, 2, 0, HALF)],
    [(0, 2, 0, HALF)],
]


def tile_splatinformationflow_pb_v_kernel(
    tc, token_embeddings, splat_influences, decoded, gate_W, gate_b, flow, z, grad_out, out_0, out_1
):
    nc = tc.nc

    by_group = "(g p j) w -> p g j w"
    x_hbm = token_embeddings.flatten_outer_dims().rearrange(by_group, p=P, j=PACK)
    z_hbm = z.flatten_outer_dims().rearrange(by_group, p=P, j=PACK)
    flow_hbm = flow.flatten_outer_dims().rearrange(by_group, p=P, j=PACK)
    grad_hbm = grad_out.flatten_outer_dims().rearrange(by_group, p=P, j=PACK)
    dx_hbm = out_0.flatten_outer_dims().rearrange(by_group, p=P, j=PACK)
    w_hbm = gate_W.rearrange("(t p) o -> p t o", p=P)
    dw_hbm = out_1.rearrange("(t p) o -> p t o", p=P)

    with ExitStack() as ctx:
        keep = ctx.enter_context(tc.tile_pool(name="keep", bufs=1))
        laced_pool = ctx.enter_context(tc.tile_pool(name="laced_pool", bufs=3))
        turned_pool = ctx.enter_context(tc.tile_pool(name="turned_pool", bufs=3))
        turn_psum = ctx.enter_context(tc.psum_pool(name="turn_psum", bufs=2))
        dx_psum = ctx.enter_context(tc.psum_pool(name="dx_psum", bufs=2))
        dw_psum = ctx.enter_context(tc.psum_pool(name="dw_psum", bufs=4))

        identity = keep.tile([P, P], F32, name="identity")
        make_identity(nc, identity[:])
        minus_half = keep.tile([P, 1], F32, name="minus_half")
        nc.vector.memset(minus_half[:], -0.5)
        table_warmer = keep.tile([P, 1], F32, name="table_warmer")
        nc.scalar.activation(out=table_warmer[:], in_=minus_half[:], func=ACT.Sigmoid)

        w_raw = keep.tile([P, W_TILES, FEATURES], BF16, name="w_raw")
        z_sb = [keep.tile([P, nj, nw], F32, name="z_sb%d" % panel) for panel, (g, j0, nj, w0, nw) in enumerate(PANELS)]
        flow_sb = [keep.tile([P, nj, nw], F32, name="flow_sb%d" % panel) for panel, (g, j0, nj, w0, nw) in enumerate(PANELS)]
        dz_sb = [keep.tile([P, PACK, FEATURES], BF16, name="dz_sb%d" % g) for g in range(GROUPS)]
        x_sb = [keep.tile([P, PACK, FEATURES], BF16, name="x_sb%d" % g) for g in range(GROUPS)]

        def code_tile(name, width):
            return keep.tile([P, width], U32, name=name, align_bytes=64)

        def scale_tile(name, width):
            return keep.tile([P, width], U8, name=name, align_bytes=64)

        w_codes = [code_tile("w_codes%d" % h, FEATURES) for h in range(HALVES)]
        w_scales = [scale_tile("w_scales%d" % h, FEATURES) for h in range(HALVES)]
        x_codes = [code_tile("x_codes%d" % g, FEATURES) for g in range(GROUPS)]
        x_scales = [scale_tile("x_scales%d" % g, FEATURES) for g in range(GROUPS)]
        dzk_tok_codes = [[code_tile("dzk_tok_codes%d_%d" % (g, h), HALF) for h in range(HALVES)] for g in range(GROUPS)]
        dzk_tok_scales = [[scale_tile("dzk_tok_scales%d_%d" % (g, h), HALF) for h in range(HALVES)] for g in range(GROUPS)]
        dzk_feat_codes = [
            [[code_tile("dzk_feat_codes%d_%d_%d" % (g, a, h), 2 * P) for h in range(HALVES)] for a in range(2)]
            for g in range(GROUPS)
        ]
        dzk_feat_scales = [
            [[scale_tile("dzk_feat_scales%d_%d_%d" % (g, a, h), 2 * P) for h in range(HALVES)] for a in range(2)]
            for g in range(GROUPS)
        ]

        dx_stage = {}
        for g in range(2):
            for a in range(2):
                dx_stage[(g, a)] = flow_sb[2 * g + a][:]
        dx_stage[(2, 0)] = flow_sb[4][:].rearrange("p j w -> p (j w)").rearrange("p (i c) -> p i c", i=2)
        dx_stage[(2, 1)] = z_sb[4][:].rearrange("p j w -> p (j w)").rearrange("p (i c) -> p i c", i=2)
        dw_stage = {}
        for h in range(HALVES):
            for q in range(W_TILES // 2):
                dw_stage[(q, h)] = z_sb[2 * h + q // 2][:, q % 2, :].rearrange("p (i c) -> p i c", i=2)

        turn_bank = {}
        turned = {}
        laced = {}
        dx_acc = {}
        dw_acc = {}


        def load_part(tiles, hbm, panel, js, nj, ws, nw):
            g, j0, w0 = PANELS[panel][0], PANELS[panel][1], PANELS[panel][3]
            nc.sync.dma_start(
                out=tiles[panel][:, js : js + nj, ws : ws + nw],
                in_=hbm[:, g, j0 + js : j0 + js + nj, w0 + ws : w0 + ws + nw],
            )

        def load_piece(tiles, hbm, panel, piece):
            js, nj, ws, nw = PIECES[panel][piece]
            load_part(tiles, hbm, panel, js, nj, ws, nw)

        def load_panel(tiles, hbm, panel):
            load_part(tiles, hbm, panel, 0, PANELS[panel][2], 0, PANELS[panel][4])

        def load_grad(g, a):
            nc.sync.dma_start(out=dz_sb[g][:, 2 * a : 2 * a + 2, :], in_=grad_hbm[:, g, 2 * a : 2 * a + 2, :])

        def load_x(g):
            nc.sync.dma_start(out=x_sb[g][:], in_=x_hbm[:, g, :, :])

        def load_w(t):
            nc.sync.dma_start(out=w_raw[:, t : t + 2, :], in_=w_hbm[:, t : t + 2, :])


        def z_piece(panel, piece):
            js, nj, ws, nw = PIECES[panel][piece]
            return z_sb[panel][:, js : js + nj, ws : ws + nw]

        def sigmoid(panel, piece):
            nc.scalar.activation(out=z_piece(panel, piece), in_=z_piece(panel, piece), func=ACT.Sigmoid)

        def square(panel, piece):
            nc.scalar.activation(out=z_piece(panel, piece), in_=z_piece(panel, piece), func=ACT.Square, bias=minus_half[:])

        def times_flow(panel, piece):
            js, nj, ws, nw = PIECES[panel][piece]
            nc.vector.scalar_tensor_tensor(
                out=z_piece(panel, piece),
                in0=z_piece(panel, piece),
                scalar=0.25,
                in1=flow_sb[panel][:, js : js + nj, ws : ws + nw],
                op0=ALU.subtract,
                op1=ALU.mult,
            )

        def times_grad(panel, piece):
            g, j0, w0 = PANELS[panel][0], PANELS[panel][1], PANELS[panel][3]
            js, nj, ws, nw = PIECES[panel][piece]
            spot = dz_sb[g][:, j0 + js : j0 + js + nj, w0 + ws : w0 + ws + nw]
            nc.vector.scalar_tensor_tensor(
                out=spot, in0=z_piece(panel, piece), scalar=-1.0, in1=spot, op0=ALU.mult, op1=ALU.mult
            )


        def turn(key, words, first, h):
            turn_bank[key] = turn_psum.tile([P, 2, 2, P], F32, name="turn_bank", tag="turn_bank")
            for i in range(2):
                for u in range(2):
                    nc.tensor.transpose(
                        turn_bank[key][:, i, u, :], words[:, first + i, WORDS * h + u : WORDS * (h + 1) : 2], identity[:]
                    )

        def copy_turned(key):
            turned[key] = turned_pool.tile([P, 2, P, PACK], BF16, name="turned", tag="turned", align_bytes=64)
            nc.scalar.copy(out=turned[key][:].bitcast(F32), in_=turn_bank[key][:].rearrange("m i u r -> m i r u"))

        def quantize_turned(key, code_words, scale_bytes, fmt):
            nc.vector.quantize_mx(
                out=code_words.bitcast(fmt), scales=scale_bytes, in_=turned[key][:].rearrange("m i r v -> m (i r v)")
            )

        def turn_w(h, q):
            turn(("w", h, q), w_raw[:].bitcast(F32), 2 * q, h)

        def copy_w(h, q):
            copy_turned(("w", h, q))

        def quantize_w(h, q):
            cols = slice(2 * P * q, 2 * P * (q + 1))
            quantize_turned(("w", h, q), w_codes[h][:, cols], w_scales[h][:, cols], E4M3)

        def turn_dz(g, a, h):
            turn((g, a, h), dz_sb[g][:].bitcast(F32), 2 * a, h)

        def copy_dz(g, a, h):
            copy_turned((g, a, h))

        def quantize_dz(g, a, h):
            quantize_turned((g, a, h), dzk_feat_codes[g][a][h][:], dzk_feat_scales[g][a][h][:], E5M2)


        def lace(key, by_slot):
            laced[key] = laced_pool.tile([P, HALF, PACK], BF16, name="laced", tag="laced", align_bytes=64)
            nc.vector.tensor_copy(out=laced[key][:], in_=by_slot.rearrange("p j w -> p w j"))

        def quantize_laced(key, code_words, scale_bytes, fmt):
            nc.vector.quantize_mx(
                out=code_words.bitcast(fmt), scales=scale_bytes, in_=laced[key][:].rearrange("p w j -> p (w j)")
            )

        def lace_x(g, h):
            lace(("x", g, h), x_sb[g][:, :, HALF * h : HALF * (h + 1)])

        def quantize_x(g, h):
            cols = slice(HALF * h, HALF * (h + 1))
            quantize_laced(("x", g, h), x_codes[g][:, cols], x_scales[g][:, cols], E4M3)

        def lace_dz(g, h):
            lace(("dz", g, h), dz_sb[g][:, :, HALF * h : HALF * (h + 1)])

        def quantize_laced_dz(g, h):
            quantize_laced(("dz", g, h), dzk_tok_codes[g][h][:], dzk_tok_scales[g][h][:], E5M2)


        def drain(out, acc, on_vector):
            if on_vector:
                nc.vector.tensor_copy(out=out, in_=acc)
            else:
                nc.scalar.copy(out=out, in_=acc)

        def mm_dx(g, a, i, n, h):
            if h == 0:
                dx_acc[(g, a, i, n)] = dx_psum.tile([P, HALF], F32, name="dx_acc", tag="dx_acc")
            tokens = slice(P * i, P * (i + 1))
            cols = slice(HALF * n, HALF * (n + 1))
            nc.tensor.matmul_mx(
                out=dx_acc[(g, a, i, n)][:],
                lhsT=dzk_feat_codes[g][a][h][:, tokens].bitcast(E5M2),
                lhsT_scale=dzk_feat_scales[g][a][h][:, tokens],
                rhs=w_codes[h][:, cols].bitcast(E4M3),
                rhs_scale=w_scales[h][:, cols],
                start=(h == 0),
                stop=(h == HALVES - 1),
            )

        def mm_dx_pass(g, a, i, h):
            for n in range(HALVES):
                mm_dx(g, a, i, n, h)

        def mm_dx_whole(g, a, i):
            for n in range(HALVES):
                for h in range(HALVES):
                    mm_dx(g, a, i, n, h)

        def drain_dx(g, a, i, share):
            for n in range(HALVES):
                drain(dx_stage[(g, a)][:, i, HALF * n : HALF * (n + 1)], dx_acc[(g, a, i, n)][:], share and n == 1)

        def store_dx(g, a):
            nc.sync.dma_start(out=dx_hbm[:, g, 2 * a : 2 * a + 2, :], in_=dx_stage[(g, a)])

        def store_dx_slot(g, a, i):
            nc.sync.dma_start(out=dx_hbm[:, g, 2 * a + i, :], in_=dx_stage[(g, a)][:, i, :])

        def mm_dw(t, h, g):
            if g == 0:
                dw_acc[(t, h)] = dw_psum.tile([P, HALF], F32, name="dw_acc", tag="dw_acc")
            cols = slice(P * t, P * (t + 1))
            nc.tensor.matmul_mx(
                out=dw_acc[(t, h)][:],
                lhsT=x_codes[g][:, cols].bitcast(E4M3),
                lhsT_scale=x_scales[g][:, cols],
                rhs=dzk_tok_codes[g][h][:].bitcast(E5M2),
                rhs_scale=dzk_tok_scales[g][h][:],
                start=(g == 0),
                stop=(g == GROUPS - 1),
            )

        def drain_dw(t, h, on_vector):
            drain(dw_stage[(t // 2, h)][:, t % 2, :], dw_acc[(t, h)][:], on_vector)

        def store_dw_pair(q, h):
            nc.sync.dma_start(out=dw_hbm[:, 2 * q : 2 * q + 2, HALF * h : HALF * (h + 1)], in_=dw_stage[(q, h)])

        def store_dw(t, h):
            nc.sync.dma_start(out=dw_hbm[:, t, HALF * h : HALF * (h + 1)], in_=dw_stage[(t // 2, h)][:, t % 2, :])

        held = range(W_TILES // 2)
        late = range(W_TILES // 2, W_TILES)

        with tc.manual_schedule():
            load_piece(z_sb, z_hbm, 0, 0)
            load_piece(flow_sb, flow_hbm, 0, 0)
            load_grad(0, 0)
            load_x(0)
            for piece in (1, 2):
                load_piece(z_sb, z_hbm, 0, piece)
                load_piece(flow_sb, flow_hbm, 0, piece)
            load_panel(z_sb, z_hbm, 1)
            load_panel(flow_sb, flow_hbm, 1)
            load_grad(0, 1)
            for t in range(0, W_TILES, 2):
                load_w(t)
            for a in range(2):
                load_panel(z_sb, z_hbm, 2 + a)
                load_panel(flow_sb, flow_hbm, 2 + a)
                load_grad(1, a)
                if a == 0:
                    load_x(1)
            load_panel(z_sb, z_hbm, 4)
            load_panel(flow_sb, flow_hbm, 4)
            load_grad(2, 0)
            load_grad(2, 1)
            load_x(2)
            for panel in (5, 6):
                load_panel(z_sb, z_hbm, panel)
                load_panel(flow_sb, flow_hbm, panel)

            for piece in range(3):
                sigmoid(0, piece)
                square(0, piece)
            times_flow(0, 0)
            times_grad(0, 0)
            lace_x(0, 1)
            lace_x(0, 0)
            times_flow(0, 1)
            quantize_x(0, 1)
            times_grad(0, 1)
            quantize_x(0, 0)
            times_flow(0, 2)
            times_grad(0, 2)

            sigmoid(1, 0)
            sigmoid(1, 1)
            square(1, 0)
            square(1, 1)
            times_flow(1, 0)
            times_flow(1, 1)
            times_grad(1, 0)
            for q in range(W_TILES // 2):
                for h in range(HALVES):
                    turn_w(h, q)
                    copy_w(h, q)
                    quantize_w(h, q)
                    if (q, h) == (0, 1):
                        times_grad(1, 1)
                    if (q, h) == (2, 0):
                        lace_dz(0, 1)
            quantize_laced_dz(0, 1)
            lace_dz(0, 0)

            turn_dz(0, 0, 0)
            turn_dz(0, 0, 1)
            sigmoid(2, 0)
            copy_dz(0, 0, 0)
            square(2, 0)
            copy_dz(0, 0, 1)
            sigmoid(2, 1)
            quantize_dz(0, 0, 0)
            quantize_laced_dz(0, 0)
            quantize_dz(0, 0, 1)
            mm_dx_pass(0, 0, 0, 0)
            mm_dx_pass(0, 0, 0, 1)
            turn_dz(0, 1, 0)
            drain_dx(0, 0, 0, False)
            square(2, 1)
            mm_dx_whole(0, 0, 1)
            turn_dz(0, 1, 1)
            drain_dx(0, 0, 1, False)
            mm_dw(0, 0, 0)
            mm_dw(1, 0, 0)

            times_flow(2, 0)
            times_grad(2, 0)
            lace_x(1, 0)
            times_flow(2, 1)
            quantize_x(1, 0)
            copy_dz(0, 1, 0)
            sigmoid(3, 0)
            copy_dz(0, 1, 1)
            square(3, 0)
            sigmoid(3, 1)
            quantize_dz(0, 1, 0)
            times_grad(2, 1)
            quantize_dz(0, 1, 1)
            lace_x(1, 1)
            mm_dx_pass(0, 1, 0, 0)
            turn_dz(1, 0, 0)
            mm_dx_pass(0, 1, 0, 1)
            drain_dx(0, 1, 0, False)
            square(3, 1)
            mm_dx_whole(0, 1, 1)
            drain_dx(0, 1, 1, False)
            mm_dw(2, 0, 0)
            mm_dw(3, 0, 0)
            turn_dz(1, 0, 1)

            times_flow(3, 0)
            quantize_x(1, 1)
            times_grad(3, 0)
            times_flow(3, 1)
            times_grad(3, 1)
            sigmoid(4, 0)
            copy_dz(1, 0, 0)
            square(4, 0)
            copy_dz(1, 0, 1)
            sigmoid(4, 1)
            quantize_dz(1, 0, 0)
            lace_dz(1, 0)
            quantize_dz(1, 0, 1)
            turn_dz(1, 1, 0)
            mm_dx_pass(1, 0, 0, 0)
            mm_dx_pass(1, 0, 0, 1)
            copy_dz(1, 1, 0)
            drain_dx(1, 0, 0, False)
            square(4, 1)
            mm_dx_whole(1, 0, 1)
            drain_dx(1, 0, 1, False)

            times_flow(4, 0)
            quantize_laced_dz(1, 0)
            mm_dw(0, 0, 1)
            turn_dz(1, 1, 1)
            mm_dw(1, 0, 1)
            quantize_dz(1, 1, 0)
            times_grad(4, 0)
            turn_dz(2, 0, 0)
            mm_dx_pass(1, 1, 0, 0)
            mm_dw(2, 0, 1)
            lace_x(2, 0)
            times_flow(4, 1)
            quantize_x(2, 0)
            times_grad(4, 1)
            sigmoid(5, 0)
            copy_dz(1, 1, 1)
            square(5, 0)
            sigmoid(6, 0)
            quantize_dz(1, 1, 1)
            lace_x(2, 1)
            lace_dz(2, 0)
            quantize_x(2, 1)
            quantize_laced_dz(2, 0)
            mm_dx_pass(1, 1, 0, 1)
            drain_dx(1, 1, 0, False)
            square(6, 0)
            mm_dx_whole(1, 1, 1)
            mm_dw(3, 0, 1)
            turn_dz(2, 1, 0)
            drain_dx(1, 1, 1, False)
            for g in range(2):
                for a in range(2):
                    store_dx(g, a)
            copy_dz(2, 0, 0)
            copy_dz(2, 1, 0)

            for t in held:
                mm_dw(t, 0, 2)
            times_flow(5, 0)
            quantize_dz(2, 0, 0)
            lace_dz(1, 1)
            quantize_dz(2, 1, 0)
            times_grad(5, 0)
            quantize_laced_dz(1, 1)
            times_flow(6, 0)
            times_grad(6, 0)
            mm_dx_pass(2, 0, 0, 0)
            for t in held:
                drain_dw(t, 0, False)
            for t in late:
                for g in range(GROUPS):
                    mm_dw(t, 0, g)
            for t in late:
                drain_dw(t, 0, False)
            for q in range(W_TILES // 2):
                store_dw_pair(q, 0)

            turn_dz(2, 0, 1)
            copy_dz(2, 0, 1)
            quantize_dz(2, 0, 1)
            lace_dz(2, 1)
            for t in held:
                mm_dw(t, 1, 0)
            mm_dw(0, 1, 1)
            mm_dx_pass(2, 0, 0, 1)
            drain_dx(2, 0, 0, True)
            store_dx_slot(2, 0, 0)
            mm_dw(1, 1, 1)
            mm_dw(2, 1, 1)
            mm_dx(2, 0, 1, 0, 0)
            mm_dx(2, 0, 1, 0, 1)
            mm_dw(3, 1, 1)
            mm_dx(2, 0, 1, 1, 0)
            mm_dx(2, 0, 1, 1, 1)
            quantize_laced_dz(2, 1)
            drain_dx(2, 0, 1, True)
            store_dx_slot(2, 0, 1)
            turn_dz(2, 1, 1)
            copy_dz(2, 1, 1)
            quantize_dz(2, 1, 1)
            for t in held:
                mm_dw(t, 1, 2)
            for t in held:
                drain_dw(t, 1, t % 2 == 1)
                store_dw(t, 1)
            mm_dx_whole(2, 1, 0)
            mm_dw(4, 1, 0)
            drain_dx(2, 1, 0, True)
            mm_dx_whole(2, 1, 1)
            mm_dw(4, 1, 1)
            mm_dw(4, 1, 2)
            drain_dx(2, 1, 1, True)
            store_dx_slot(2, 1, 0)
            store_dx_slot(2, 1, 1)
            for t in late[1:]:
                for g in range(GROUPS):
                    mm_dw(t, 1, g)
            for t in late:
                drain_dw(t, 1, t % 2 == 1)
                store_dw(t, 1)
